import numpy as np
import ml_dtypes


def mxq(x, axis, fmt="e4m3"):
    dtype, down = {"e4m3": (ml_dtypes.float8_e4m3fn, 7), "e5m2": (ml_dtypes.float8_e5m2, 14)}[fmt]
    v = np.moveaxis(np.asarray(x, np.float32).astype(ml_dtypes.bfloat16).astype(np.float64), axis, -1)
    blocks = v.reshape(v.shape[:-1] + (-1, 32))
    amax = np.abs(blocks).max(-1, keepdims=True)
    byte = np.maximum(np.where(amax > 0, np.frexp(amax)[1] - 1 + 127, 0) - down, 1)
    scale = np.exp2(byte - 127.0)
    codes = (blocks / scale).astype(np.float32).astype(dtype).astype(np.float64)
    return np.moveaxis((codes * scale).reshape(v.shape), -1, axis)


WIDE = False


def mx_kscale(k):
    if not WIDE:
        return np.ones(k)
    levels = np.array([10, -10, 5, -5, 0])
    a = np.random.permutation(np.resize(levels, k // 512 * 4)).reshape(k // 512, 4)
    idx = np.arange(k)
    return np.exp2(a[idx // 512, idx % 128 // 32])


BF16 = ml_dtypes.bfloat16


def bf(x):
    return np.asarray(x, np.float32).astype(BF16)


def f64(x):
    return np.asarray(x).astype(np.float64)


B, N, M, D = 2, 4096, 512, 1024

C = 1.0
SQRT_C = 1.0
EPS = 1e-10
NORM_MAX = 0.99
RAD = 0.85
SIG = 0.35


def setup_inputs():
    g = np.random.standard_normal((B, 1, D))
    g = g / np.sqrt((g * g).sum(-1, keepdims=True))
    a = RAD * np.cos(np.pi * np.random.random_sample((B, N, 1)))
    c = RAD * np.cos(np.pi * np.random.random_sample((B, M, 1)))
    x = a * g + np.random.standard_normal((B, N, D)) * SIG / np.sqrt(D)
    y = c * g + np.random.standard_normal((B, M, D)) * SIG / np.sqrt(D)
    s = mx_kscale(D)
    x[:, 3::4, :] = x[:, 3::4, :] * (s * s)
    return {"x": bf(x), "y": bf(y)}


def reference(x, y):
    x = f64(x)
    y = f64(y)
    xs = np.sum(x * x, axis=-1)
    ys = np.sum(y * y, axis=-1)
    dot = mxq(x, 2, "e4m3") @ mxq(y, 2, "e4m3").transpose(0, 2, 1)
    xs_ = xs[:, :, None]
    ys_ = ys[:, None, :]
    A = 1.0 - 2.0 * C * dot + C * ys_
    Bc = 1.0 - C * xs_
    denom = 1.0 - 2.0 * C * dot + (C * C) * xs_ * ys_
    num_sq = A * A * xs_ - 2.0 * A * Bc * dot + Bc * Bc * ys_
    diff_norm = np.sqrt(np.maximum(num_sq, 0.0)) / np.maximum(denom, EPS)
    diff_norm = np.clip(diff_norm, EPS, NORM_MAX)
    return (2.0 / SQRT_C) * np.arctanh(SQRT_C * diff_norm)

@@ -1,0 +1,305 @@
+import concourse.mybir as mybir
+from concourse.masks import make_identity
+
+F32 = mybir.dt.float32
+BF16 = mybir.dt.bfloat16
+U32 = mybir.dt.uint32
+U8 = mybir.dt.uint8
+FP8X4 = mybir.dt.float8_e4m3fn_x4
+ALU = mybir.AluOpType
+FUNC = mybir.ActivationFunctionType
+
+B, N, M, D = 2, 4096, 512, 1024
+FLOPS = 2 * B * N * M * D
+
+P = 128
+ROW_TILES = 4
+ITEM_ROWS = P * ROW_TILES
+GROUPS = N // ITEM_ROWS
+K_PASS = 4 * P
+PASSES = D // K_PASS
+HALVES = 2
+ROW_WORDS = D // 2
+OUT_COLS = ROW_TILES * M
+
+NORM_MAX = 0.99
+COSH_MAX = (1.0 + NORM_MAX * NORM_MAX) / (1.0 - NORM_MAX * NORM_MAX)
+OUTSIDE = 1024.0
+TINY = 1e-30
+
+LOG_BLOCK = 4
+
+
+def tile_hyperbolicdistancelayer_t_kernel(tc, x, y, out):
+    nc = tc.nc
+
+    x_items = x.rearrange("b (g p t) k -> b g p (t k)", p=P, t=ROW_TILES)
+    y_items = y.rearrange("b (t p) k -> b p t k", p=P)
+    out_items = out.rearrange("b (g p t) j -> b g p (t j)", p=P, t=ROW_TILES)
+
+    items = []
+    for b in range(B):
+        items.append(("y", b, 0))
+        for g in range(GROUPS):
+            items.append(("x", b, g))
+
+    with (
+        tc.tile_pool(name="const", bufs=1) as const,
+        tc.tile_pool(name="raw_pool", bufs=5) as raw_pool,
+        tc.tile_pool(name="grouped_pool", bufs=2) as grouped_pool,
+        tc.tile_pool(name="mx_pool", bufs=2) as mx_pool,
+        tc.tile_pool(name="small", bufs=4) as small,
+        tc.tile_pool(name="rows_pool", bufs=2) as rows_pool,
+        tc.tile_pool(name="z_pool", bufs=8) as z_pool,
+        tc.tile_pool(name="root_pool", bufs=3) as root_pool,
+        tc.psum_pool(name="turned_pool", bufs=4) as turned_pool,
+        tc.psum_pool(name="dot_pool", bufs=4) as dot_pool,
+        tc.manual_schedule(),
+    ):
+        identity = const.tile([P, P], F32)
+        make_identity(nc, identity[:])
+        minus_one = const.tile([P, 1], F32)
+        nc.vector.memset(minus_one[:], -1.0)
+        squares = const.tile([P, ROW_TILES * D], BF16)
+
+        raw = {}
+        sumsq = {}
+        turned = {}
+        grouped = {}
+        codes = {}
+        scales = {}
+        a_of = {}
+        g_of = {}
+        spread = {}
+        y_of = {}
+        dots = {}
+        z_of = {}
+        root = {}
+
+        def kind(m):
+            return items[m][0] if 0 <= m < len(items) else "none"
+
+        def load(m):
+            if kind(m) == "none":
+                return
+            what, b, g = items[m]
+            rows = raw_pool.tile([P, ROW_TILES * D], BF16)
+            raw[m] = rows
+            if what == "x":
+                nc.sync.dma_start(out=rows[:], in_=x_items[b, g])
+            else:
+                nc.sync.dma_start(
+                    out=rows[:].rearrange("p (t k) -> p t k", t=ROW_TILES), in_=y_items[b]
+                )
+
+        def sum_squares(m):
+            if kind(m) == "none":
+                return
+            sums = small.tile([P, ROW_TILES], F32)
+            sumsq[m] = sums
+            for t in range(ROW_TILES):
+                cols = slice(t * D, (t + 1) * D)
+                nc.scalar.activation(
+                    out=squares[:, cols],
+                    in_=raw[m][:, cols],
+                    func=FUNC.Square,
+                    accum_out=sums[:, t : t + 1],
+                )
+
+        def transpose(m):
+            if kind(m) == "none":
+                return
+            words = raw[m][:].bitcast(F32)
+            turned[m] = []
+            for t in range(ROW_TILES):
+                bank = turned_pool.tile([P, PASSES, HALVES, P], F32)
+                turned[m].append(bank)
+                for c in range(PASSES):
+                    for u in range(HALVES):
+                        first = t * ROW_WORDS + (c * HALVES + u) * P
+                        nc.tensor.transpose(
+                            bank[:, c, u, :], words[:, first : first + P], identity[:]
+                        )
+
+        def regroup(m):
+            if kind(m) == "none":
+                return
+            values = grouped_pool.tile([P, ROW_TILES * D], BF16, align_bytes=64)
+            grouped[m] = values
+            if kind(m) == "x":
+                order = "q (t c r u) -> q t c r u"
+            else:
+                order = "q (c t r u) -> q t c r u"
+            places = values[:].bitcast(F32).rearrange(
+                order, t=ROW_TILES, c=PASSES, r=P, u=HALVES
+            )
+            for t in range(ROW_TILES):
+                nc.vector.tensor_copy(
+                    out=places[:, t], in_=turned[m][t][:].rearrange("q c u r -> q c r u")
+                )
+
+        def quantise(m):
+            if kind(m) == "none":
+                return
+            tag = kind(m)
+            packed = mx_pool.tile([P, ROW_TILES * D // 4], U32, align_bytes=64, tag=tag + "_codes")
+            plane = mx_pool.tile([P, ROW_TILES * D // 4], U8, align_bytes=64, tag=tag + "_scales")
+            codes[m] = packed
+            scales[m] = plane
+            nc.vector.quantize_mx(
+                out=packed[:].bitcast(FP8X4), scales=plane[:], in_=grouped[m][:]
+            )
+
+        def row_factors(m):
+            if kind(m) == "none":
+                return
+            v = sumsq[m]
+            a = small.tile([P, ROW_TILES], F32)
+            h = small.tile([P, ROW_TILES], F32)
+            h_out = small.tile([P, ROW_TILES], F32)
+            g = small.tile([P, ROW_TILES], F32)
+            a_of[m] = a
+            g_of[m] = g
+            nc.vector.tensor_scalar(
+                out=a[:], in0=v[:], scalar1=0.5, scalar2=0.5, op0=ALU.mult, op1=ALU.add
+            )
+            nc.vector.tensor_scalar(
+                out=h[:], in0=v[:], scalar1=-0.5, scalar2=0.5, op0=ALU.mult, op1=ALU.add
+            )
+            nc.vector.tensor_scalar(
+                out=h_out[:],
+                in0=v[:],
+                scalar1=0.5 / OUTSIDE,
+                scalar2=-0.5 / OUTSIDE,
+                op0=ALU.mult,
+                op1=ALU.add,
+            )
+            nc.vector.scalar_tensor_tensor(
+                out=h[:], in0=h_out[:], scalar=TINY, in1=h[:], op0=ALU.max, op1=ALU.max
+            )
+            nc.vector.reciprocal(out=g[:], in_=h[:])
+
+        def spread_over_partitions(m):
+            if kind(m) != "y":
+                return
+            spread[m] = []
+            for column in (a_of[m], g_of[m]):
+                bank = turned_pool.tile([P, PASSES, HALVES, P], F32)
+                spread[m].append(bank)
+                flat = bank[:].rearrange("p c u r -> p (c u r)")
+                for t in range(ROW_TILES):
+                    nc.tensor.matmul(
+                        out=flat[:, t * P : (t + 1) * P],
+                        lhsT=column[:, t : t + 1].to_broadcast([P, P]),
+                        rhs=identity[:],
+                        start=True,
+                        stop=True,
+                    )
+
+        def keep_rows(m):
+            if kind(m) != "y":
+                return
+            a_row = rows_pool.tile([P, M], F32)
+            g_row = rows_pool.tile([P, M], F32)
+            nc.vector.tensor_copy(out=a_row[:], in_=spread[m][0][:].rearrange("p c u r -> p (c u r)"))
+            nc.vector.tensor_copy(out=g_row[:], in_=spread[m][1][:].rearrange("p c u r -> p (c u r)"))
+            y_of[items[m][1]] = (codes[m], scales[m], a_row, g_row)
+
+        def multiply(m):
+            if kind(m) != "x":
+                return
+            y_codes, y_scales = y_of[items[m][1]][0:2]
+            dots[m] = []
+            for t in range(ROW_TILES):
+                acc = dot_pool.tile([P, M], F32)
+                dots[m].append(acc)
+                for c in range(PASSES):
+                    x_cols = slice((t * PASSES + c) * P, (t * PASSES + c + 1) * P)
+                    y_cols = slice(c * M, (c + 1) * M)
+                    nc.tensor.matmul_mx(
+                        out=acc[:],
+                        lhsT=codes[m][:, x_cols].bitcast(FP8X4),
+                        lhsT_scale=scales[m][:, x_cols],
+                        rhs=y_codes[:, y_cols].bitcast(FP8X4),
+                        rhs_scale=y_scales[:, y_cols],
+                        start=(c == 0),
+                        stop=(c == PASSES - 1),
+                    )
+
+        def numerator(m):
+            if kind(m) != "x":
+                return
+            a_row = y_of[items[m][1]][2]
+            z = z_pool.tile([P, OUT_COLS], F32)
+            z_of[m] = z
+            for t in range(ROW_TILES):
+                nc.vector.scalar_tensor_tensor(
+                    out=z[:, t * M : (t + 1) * M],
+                    in0=a_row[:],
+                    scalar=a_of[m][:, t : t + 1],
+                    in1=dots[m][t][:],
+                    op0=ALU.mult,
+                    op1=ALU.subtract,
+                )
+
+        def cosh_clipped(m):
+            if kind(m) != "x":
+                return
+            g_row = y_of[items[m][1]][3]
+            z = z_of[m]
+            for t in range(ROW_TILES):
+                cols = slice(t * M, (t + 1) * M)
+                nc.vector.scalar_tensor_tensor(
+                    out=z[:, cols],
+                    in0=z[:, cols],
+                    scalar=g_of[m][:, t : t + 1],
+                    in1=g_row[:],
+                    op0=ALU.mult,
+                    op1=ALU.mult,
+                )
+            nc.vector.tensor_scalar(
+                out=z[:], in0=z[:], scalar1=1.0, scalar2=COSH_MAX, op0=ALU.max, op1=ALU.min
+            )
+
+        def square_root(m):
+            if kind(m) != "x":
+                return
+            r = root_pool.tile([P, OUT_COLS], F32)
+            root[m] = r
+            halves = (slice(0, OUT_COLS // 2), slice(OUT_COLS // 2, OUT_COLS))
+            for cols in halves:
+                nc.scalar.activation(out=r[:, cols], in_=z_of[m][:, cols], func=FUNC.Square)
+            for cols in halves:
+                nc.scalar.activation(
+                    out=r[:, cols], in_=r[:, cols], func=FUNC.Sqrt, bias=minus_one[:, 0:1]
+                )
+
+        def add_root(m):
+            if kind(m) != "x":
+                return
+            z = z_of[m]
+            nc.vector.tensor_tensor(out=z[:], in0=z[:], in1=root[m][:], op=ALU.add)
+
+        def logarithms(last):
+            if kind(last) != "x" or (items[last][2] + 1) % LOG_BLOCK != 0:
+                return
+            for m in range(last - LOG_BLOCK + 1, last + 1):
+                z = z_of[m]
+                nc.scalar.activation(out=z[:], in_=z[:], func=FUNC.Ln)
+                nc.scalar.dma_start(out=out_items[items[m][1], items[m][2]], in_=z[:])
+
+        for s in range(-4, len(items) + 2):
+            keep_rows(s)
+            load(s + 4)
+            transpose(s + 2)
+            quantise(s + 1)
+            row_factors(s + 1)
+            numerator(s)
+            multiply(s + 1)
+            square_root(s - 1)
+            sum_squares(s + 3)
+            regroup(s + 2)
+            spread_over_partitions(s + 1)
+            cosh_clipped(s)
+            add_root(s - 2)
+            logarithms(s - 2)

@@ -13,54 +13,71 @@ B, N, M, D = 2, 4096, 512, 1024
 FLOPS = 2 * B * N * M * D
 
 P = 128
-ROW_TILES = 4
-ITEM_ROWS = P * ROW_TILES
+TILES = 4
+ITEM_ROWS = P * TILES
 GROUPS = N // ITEM_ROWS
 K_PASS = 4 * P
 PASSES = D // K_PASS
 HALVES = 2
 ROW_WORDS = D // 2
-OUT_COLS = ROW_TILES * M
+OUT_COLS = TILES * M
+HALF = OUT_COLS // 2
 
 NORM_MAX = 0.99
 COSH_MAX = (1.0 + NORM_MAX * NORM_MAX) / (1.0 - NORM_MAX * NORM_MAX)
 OUTSIDE = 1024.0
 TINY = 1e-30
 
-LOG_BLOCK = 4
+LOG_BLOCKS = (2, 4, 4, 4, 2)
+LAG = 2
+BUD = 24
+BUD2 = 48
+LNC = 4
 
 
 def tile_hyperbolicdistancelayer_t_kernel(tc, x, y, out):
     nc = tc.nc
 
-    x_items = x.rearrange("b (g p t) k -> b g p (t k)", p=P, t=ROW_TILES)
+    x_items = x.rearrange("b (g p t) k -> b g p (t k)", p=P, t=TILES)
     y_items = y.rearrange("b (t p) k -> b p t k", p=P)
-    out_items = out.rearrange("b (g p t) j -> b g p (t j)", p=P, t=ROW_TILES)
+    out_items = out.rearrange("b (g p t) j -> b g p (t j)", p=P, t=TILES)
 
     items = []
     for b in range(B):
         items.append(("y", b, 0))
         for g in range(GROUPS):
             items.append(("x", b, g))
+    x_order = [m for m in range(len(items)) if items[m][0] == "x"]
+
+    table_work = []
+    first = 0
+    for size in LOG_BLOCKS:
+        block = list(range(first, first + size))
+        first += size
+        table_work.extend(("sqrt", n, half) for n in block for half in range(2))
+        table_work.extend(("ln", n, t) for n in block for t in range(TILES))
 
     with (
         tc.tile_pool(name="const", bufs=1) as const,
-        tc.tile_pool(name="raw_pool", bufs=5) as raw_pool,
+        tc.tile_pool(name="raw_pool", bufs=4) as raw_pool,
         tc.tile_pool(name="grouped_pool", bufs=2) as grouped_pool,
         tc.tile_pool(name="mx_pool", bufs=2) as mx_pool,
         tc.tile_pool(name="small", bufs=4) as small,
         tc.tile_pool(name="rows_pool", bufs=2) as rows_pool,
-        tc.tile_pool(name="z_pool", bufs=8) as z_pool,
-        tc.tile_pool(name="root_pool", bufs=3) as root_pool,
-        tc.psum_pool(name="turned_pool", bufs=4) as turned_pool,
-        tc.psum_pool(name="dot_pool", bufs=4) as dot_pool,
+        tc.tile_pool(name="z_pool", bufs=9) as z_pool,
+        tc.tile_pool(name="root_pool", bufs=8) as root_pool,
+        tc.tile_pool(name="out_pool", bufs=2) as out_pool,
+        tc.psum_pool(name="turned_pool", bufs=2) as turned_pool,
+        tc.psum_pool(name="dot_pool", bufs=2) as dot_pool,
+        tc.psum_pool(name="spread_pool", bufs=1) as spread_pool,
+        tc.psum_pool(name="sum_pool", bufs=3) as sum_pool,
         tc.manual_schedule(),
     ):
         identity = const.tile([P, P], F32)
         make_identity(nc, identity[:])
         minus_one = const.tile([P, 1], F32)
         nc.vector.memset(minus_one[:], -1.0)
-        squares = const.tile([P, ROW_TILES * D], BF16)
+        squares = const.tile([P, TILES * D], BF16)
 
         raw = {}
         sumsq = {}
@@ -69,12 +86,16 @@ def tile_hyperbolicdistancelayer_t_kernel(tc, x, y, out):
         codes = {}
         scales = {}
         a_of = {}
+        h_of = {}
         g_of = {}
-        spread = {}
-        y_of = {}
+        a_row = {}
+        a_bank = {}
+        g_bank = {}
         dots = {}
         z_of = {}
         root = {}
+        out_of = {}
+        y_of = {}
 
         def kind(m):
             return items[m][0] if 0 <= m < len(items) else "none"
@@ -83,223 +104,279 @@ def tile_hyperbolicdistancelayer_t_kernel(tc, x, y, out):
             if kind(m) == "none":
                 return
             what, b, g = items[m]
-            rows = raw_pool.tile([P, ROW_TILES * D], BF16)
+            rows = raw_pool.tile([P, TILES * D], BF16)
             raw[m] = rows
             if what == "x":
                 nc.sync.dma_start(out=rows[:], in_=x_items[b, g])
             else:
                 nc.sync.dma_start(
-                    out=rows[:].rearrange("p (t k) -> p t k", t=ROW_TILES), in_=y_items[b]
+                    out=rows[:].rearrange("p (t k) -> p t k", t=TILES), in_=y_items[b]
                 )
 
-        def sum_squares(m):
+        def sum_squares(m, t):
             if kind(m) == "none":
                 return
-            sums = small.tile([P, ROW_TILES], F32)
-            sumsq[m] = sums
-            for t in range(ROW_TILES):
-                cols = slice(t * D, (t + 1) * D)
-                nc.scalar.activation(
-                    out=squares[:, cols],
-                    in_=raw[m][:, cols],
-                    func=FUNC.Square,
-                    accum_out=sums[:, t : t + 1],
-                )
+            if t == 0:
+                sums = small.tile([P, TILES], F32)
+                sumsq[m] = sums
+            cols = slice(t * D, (t + 1) * D)
+            nc.scalar.activation(
+                out=squares[:, cols],
+                in_=raw[m][:, cols],
+                func=FUNC.Square,
+                accum_out=sumsq[m][:, t : t + 1],
+            )
 
-        def transpose(m):
+        def transpose(m, t):
             if kind(m) == "none":
                 return
             words = raw[m][:].bitcast(F32)
-            turned[m] = []
-            for t in range(ROW_TILES):
-                bank = turned_pool.tile([P, PASSES, HALVES, P], F32)
-                turned[m].append(bank)
-                for c in range(PASSES):
-                    for u in range(HALVES):
-                        first = t * ROW_WORDS + (c * HALVES + u) * P
-                        nc.tensor.transpose(
-                            bank[:, c, u, :], words[:, first : first + P], identity[:]
-                        )
+            bank = turned_pool.tile([P, PASSES, HALVES, P], F32)
+            turned[m, t] = bank
+            for c in range(PASSES):
+                for u in range(HALVES):
+                    first = t * ROW_WORDS + (c * HALVES + u) * P
+                    nc.tensor.transpose(bank[:, c, u, :], words[:, first : first + P], identity[:])
 
-        def regroup(m):
+        def regroup(m, t):
             if kind(m) == "none":
                 return
-            values = grouped_pool.tile([P, ROW_TILES * D], BF16, align_bytes=64)
-            grouped[m] = values
-            if kind(m) == "x":
-                order = "q (t c r u) -> q t c r u"
-            else:
-                order = "q (c t r u) -> q t c r u"
-            places = values[:].bitcast(F32).rearrange(
-                order, t=ROW_TILES, c=PASSES, r=P, u=HALVES
+            if t == 0:
+                values = grouped_pool.tile([P, TILES * D], BF16, align_bytes=64)
+                grouped[m] = values
+            order = "q (t c r u) -> q t c r u" if kind(m) == "y" else "q (c t r u) -> q t c r u"
+            places = grouped[m][:].bitcast(F32).rearrange(order, t=TILES, c=PASSES, r=P, u=HALVES)
+            nc.vector.tensor_copy(
+                out=places[:, t], in_=turned[m, t][:].rearrange("q c u r -> q c r u")
             )
-            for t in range(ROW_TILES):
-                nc.vector.tensor_copy(
-                    out=places[:, t], in_=turned[m][t][:].rearrange("q c u r -> q c r u")
-                )
 
         def quantise(m):
             if kind(m) == "none":
                 return
             tag = kind(m)
-            packed = mx_pool.tile([P, ROW_TILES * D // 4], U32, align_bytes=64, tag=tag + "_codes")
-            plane = mx_pool.tile([P, ROW_TILES * D // 4], U8, align_bytes=64, tag=tag + "_scales")
+            packed = mx_pool.tile([P, TILES * D // 4], U32, align_bytes=64, tag=tag + "_codes")
+            plane = mx_pool.tile([P, TILES * D // 4], U8, align_bytes=64, tag=tag + "_scales")
             codes[m] = packed
             scales[m] = plane
-            nc.vector.quantize_mx(
-                out=packed[:].bitcast(FP8X4), scales=plane[:], in_=grouped[m][:]
-            )
+            nc.vector.quantize_mx(out=packed[:].bitcast(FP8X4), scales=plane[:], in_=grouped[m][:])
 
-        def row_factors(m):
+        def factors(m, stage):
             if kind(m) == "none":
                 return
             v = sumsq[m]
-            a = small.tile([P, ROW_TILES], F32)
-            h = small.tile([P, ROW_TILES], F32)
-            h_out = small.tile([P, ROW_TILES], F32)
-            g = small.tile([P, ROW_TILES], F32)
-            a_of[m] = a
-            g_of[m] = g
+            if stage == 0:
+                h = small.tile([P, TILES], F32)
+                h_out = small.tile([P, TILES], F32)
+                h_of[m] = (h, h_out)
+                nc.vector.tensor_scalar(
+                    out=h[:], in0=v[:], scalar1=-0.5, scalar2=0.5, op0=ALU.mult, op1=ALU.add
+                )
+                if kind(m) == "y":
+                    a = small.tile([P, TILES], F32, tag="y_a")
+                    a_of[m] = a
+                    nc.vector.tensor_scalar(
+                        out=a[:], in0=v[:], scalar1=0.5, scalar2=0.5, op0=ALU.mult, op1=ALU.add
+                    )
+            elif stage == 1:
+                nc.vector.tensor_scalar(
+                    out=h_of[m][1][:],
+                    in0=v[:],
+                    scalar1=0.5 / OUTSIDE,
+                    scalar2=-0.5 / OUTSIDE,
+                    op0=ALU.mult,
+                    op1=ALU.add,
+                )
+            elif stage == 2:
+                h, h_out = h_of[m]
+                nc.vector.scalar_tensor_tensor(
+                    out=h[:], in0=h_out[:], scalar=TINY, in1=h[:], op0=ALU.max, op1=ALU.max
+                )
+            else:
+                g = small.tile([P, TILES], F32, tag=kind(m) + "_g")
+                g_of[m] = g
+                nc.vector.reciprocal(out=g[:], in_=h_of[m][0][:])
+                if kind(m) == "y":
+                    y_of[items[m][1]] = m
+
+        def spread(m, column, tag):
+            bank = spread_pool.tile([P, ITEM_ROWS], F32)
+            for t in range(TILES):
+                nc.tensor.transpose(
+                    bank[:, t * P : (t + 1) * P],
+                    column[:, t : t + 1].to_broadcast([P, P]),
+                    identity[:],
+                )
+            return bank
+
+        def spread_sums(m):
+            if kind(m) == "x":
+                a_bank[m] = spread(m, sumsq[m], "a_bank")
+
+        def keep_a_row(m):
+            if kind(m) != "x":
+                return
+            row = rows_pool.tile([P, ITEM_ROWS], F32)
+            a_row[m] = row
             nc.vector.tensor_scalar(
-                out=a[:], in0=v[:], scalar1=0.5, scalar2=0.5, op0=ALU.mult, op1=ALU.add
+                out=row[:], in0=a_bank[m][:], scalar1=0.5, scalar2=0.5, op0=ALU.mult, op1=ALU.add
             )
-            nc.vector.tensor_scalar(
-                out=h[:], in0=v[:], scalar1=-0.5, scalar2=0.5, op0=ALU.mult, op1=ALU.add
-            )
-            nc.vector.tensor_scalar(
-                out=h_out[:],
-                in0=v[:],
-                scalar1=0.5 / OUTSIDE,
-                scalar2=-0.5 / OUTSIDE,
-                op0=ALU.mult,
-                op1=ALU.add,
-            )
+
+        def spread_g(m):
+            if kind(m) == "x":
+                g_bank[m] = spread(m, g_of[m], "g_bank")
+
+        def multiply(m, j):
+            if kind(m) != "x":
+                return
+            ym = y_of[items[m][1]]
+            acc = dot_pool.tile([P, ITEM_ROWS], F32)
+            dots[m, j] = acc
+            for c in range(PASSES):
+                y_cols = slice((j * PASSES + c) * P, (j * PASSES + c + 1) * P)
+                x_cols = slice(c * ITEM_ROWS, (c + 1) * ITEM_ROWS)
+                nc.tensor.matmul_mx(
+                    out=acc[:],
+                    lhsT=codes[ym][:, y_cols].bitcast(FP8X4),
+                    lhsT_scale=scales[ym][:, y_cols],
+                    rhs=codes[m][:, x_cols].bitcast(FP8X4),
+                    rhs_scale=scales[m][:, x_cols],
+                    start=(c == 0),
+                    stop=(c == PASSES - 1),
+                )
+
+        def numerator(m, j):
+            if kind(m) != "x":
+                return
+            ym = y_of[items[m][1]]
+            if j == 0:
+                z = z_pool.tile([P, OUT_COLS], F32)
+                z_of[m] = z
             nc.vector.scalar_tensor_tensor(
-                out=h[:], in0=h_out[:], scalar=TINY, in1=h[:], op0=ALU.max, op1=ALU.max
-            )
-            nc.vector.reciprocal(out=g[:], in_=h[:])
-
-        def spread_over_partitions(m):
-            if kind(m) != "y":
-                return
-            spread[m] = []
-            for column in (a_of[m], g_of[m]):
-                bank = turned_pool.tile([P, PASSES, HALVES, P], F32)
-                spread[m].append(bank)
-                flat = bank[:].rearrange("p c u r -> p (c u r)")
-                for t in range(ROW_TILES):
-                    nc.tensor.matmul(
-                        out=flat[:, t * P : (t + 1) * P],
-                        lhsT=column[:, t : t + 1].to_broadcast([P, P]),
-                        rhs=identity[:],
-                        start=True,
-                        stop=True,
-                    )
-
-        def keep_rows(m):
-            if kind(m) != "y":
-                return
-            a_row = rows_pool.tile([P, M], F32)
-            g_row = rows_pool.tile([P, M], F32)
-            nc.vector.tensor_copy(out=a_row[:], in_=spread[m][0][:].rearrange("p c u r -> p (c u r)"))
-            nc.vector.tensor_copy(out=g_row[:], in_=spread[m][1][:].rearrange("p c u r -> p (c u r)"))
-            y_of[items[m][1]] = (codes[m], scales[m], a_row, g_row)
-
-        def multiply(m):
-            if kind(m) != "x":
-                return
-            y_codes, y_scales = y_of[items[m][1]][0:2]
-            dots[m] = []
-            for t in range(ROW_TILES):
-                acc = dot_pool.tile([P, M], F32)
-                dots[m].append(acc)
-                for c in range(PASSES):
-                    x_cols = slice((t * PASSES + c) * P, (t * PASSES + c + 1) * P)
-                    y_cols = slice(c * M, (c + 1) * M)
-                    nc.tensor.matmul_mx(
-                        out=acc[:],
-                        lhsT=codes[m][:, x_cols].bitcast(FP8X4),
-                        lhsT_scale=scales[m][:, x_cols],
-                        rhs=y_codes[:, y_cols].bitcast(FP8X4),
-                        rhs_scale=y_scales[:, y_cols],
-                        start=(c == 0),
-                        stop=(c == PASSES - 1),
-                    )
-
-        def numerator(m):
-            if kind(m) != "x":
-                return
-            a_row = y_of[items[m][1]][2]
-            z = z_pool.tile([P, OUT_COLS], F32)
-            z_of[m] = z
-            for t in range(ROW_TILES):
-                nc.vector.scalar_tensor_tensor(
-                    out=z[:, t * M : (t + 1) * M],
-                    in0=a_row[:],
-                    scalar=a_of[m][:, t : t + 1],
-                    in1=dots[m][t][:],
-                    op0=ALU.mult,
-                    op1=ALU.subtract,
-                )
-
-        def cosh_clipped(m):
-            if kind(m) != "x":
-                return
-            g_row = y_of[items[m][1]][3]
-            z = z_of[m]
-            for t in range(ROW_TILES):
-                cols = slice(t * M, (t + 1) * M)
-                nc.vector.scalar_tensor_tensor(
-                    out=z[:, cols],
-                    in0=z[:, cols],
-                    scalar=g_of[m][:, t : t + 1],
-                    in1=g_row[:],
-                    op0=ALU.mult,
-                    op1=ALU.mult,
-                )
-            nc.vector.tensor_scalar(
-                out=z[:], in0=z[:], scalar1=1.0, scalar2=COSH_MAX, op0=ALU.max, op1=ALU.min
+                out=z_of[m][:, j * ITEM_ROWS : (j + 1) * ITEM_ROWS],
+                in0=a_row[m][:],
+                scalar=a_of[ym][:, j : j + 1],
+                in1=dots[m, j][:],
+                op0=ALU.mult,
+                op1=ALU.subtract,
             )
 
-        def square_root(m):
+        def cosh(m, j):
             if kind(m) != "x":
                 return
-            r = root_pool.tile([P, OUT_COLS], F32)
-            root[m] = r
-            halves = (slice(0, OUT_COLS // 2), slice(OUT_COLS // 2, OUT_COLS))
-            for cols in halves:
-                nc.scalar.activation(out=r[:, cols], in_=z_of[m][:, cols], func=FUNC.Square)
-            for cols in halves:
-                nc.scalar.activation(
-                    out=r[:, cols], in_=r[:, cols], func=FUNC.Sqrt, bias=minus_one[:, 0:1]
+            ym = y_of[items[m][1]]
+            cols = slice(j * ITEM_ROWS, (j + 1) * ITEM_ROWS)
+            nc.vector.scalar_tensor_tensor(
+                out=z_of[m][:, cols],
+                in0=z_of[m][:, cols],
+                scalar=g_of[ym][:, j : j + 1],
+                in1=g_bank[m][:],
+                op0=ALU.mult,
+                op1=ALU.mult,
+            )
+
+        def clip(m, half):
+            if kind(m) != "x":
+                return
+            cols = slice(half * HALF, (half + 1) * HALF)
+            nc.gpsimd.tensor_scalar(
+                out=z_of[m][:, cols],
+                in0=z_of[m][:, cols],
+                scalar1=1.0,
+                scalar2=COSH_MAX,
+                op0=ALU.max,
+                op1=ALU.min,
+            )
+
+        def square(m, half):
+            if kind(m) != "x":
+                return
+            if half == 0:
+                r = root_pool.tile([P, OUT_COLS], F32)
+                root[m] = r
+            cols = slice(half * HALF, (half + 1) * HALF)
+            nc.gpsimd.tensor_tensor(
+                out=root[m][:, cols], in0=z_of[m][:, cols], in1=z_of[m][:, cols], op=ALU.mult
+            )
+
+        def square_root(m, half):
+            cols = slice(half * HALF, (half + 1) * HALF)
+            nc.scalar.activation(
+                out=root[m][:, cols], in_=root[m][:, cols], func=FUNC.Sqrt, bias=minus_one[:, 0:1]
+            )
+
+        def logarithm(m, t):
+            bank = sum_pool.tile([P, M], F32)
+            for j in range(TILES):
+                cols = slice(j * ITEM_ROWS + t * P, j * ITEM_ROWS + (t + 1) * P)
+                place = bank[:, j * P : (j + 1) * P]
+                nc.tensor.matmul(
+                    place, lhsT=z_of[m][:, cols], rhs=identity[:], is_transpose=True, start=True, stop=False
                 )
+                nc.tensor.matmul(
+                    place, lhsT=root[m][:, cols], rhs=identity[:], is_transpose=True, start=False, stop=True
+                )
+            if t == 0:
+                result = out_pool.tile([P, OUT_COLS], F32)
+                out_of[m] = result
+            nc.scalar.activation(
+                out=out_of[m][:, t * M : (t + 1) * M], in_=bank[:], func=FUNC.Ln
+            )
+            if t == TILES - 1:
+                nc.scalar.dma_start(out=out_items[items[m][1], items[m][2]], in_=out_of[m][:])
 
-        def add_root(m):
-            if kind(m) != "x":
-                return
-            z = z_of[m]
-            nc.vector.tensor_tensor(out=z[:], in0=z[:], in1=root[m][:], op=ALU.add)
+        done = 0
+        for s in range(-5, len(items) + 6):
+            load(s + 5)
+            for half in range(2):
+                clip(s - 1, half)
+                square(s - 1, half)
+            squared = sum(1 for m in x_order if m <= s - LAG)
+            share = BUD if kind(s + 3) != "none" else BUD2
+            quarters = [[] for k in range(TILES)]
+            spent = 0
+            while spent < share and done < len(table_work) and table_work[done][1] < squared:
+                what, n, part = table_work[done]
+                m = x_order[n]
+                k = min(spent * TILES // share, TILES - 1)
+                quarters[k].append((square_root if what == "sqrt" else logarithm, m, part))
+                done += 1
+                spent += 3 if what == "sqrt" else LNC
 
-        def logarithms(last):
-            if kind(last) != "x" or (items[last][2] + 1) % LOG_BLOCK != 0:
-                return
-            for m in range(last - LOG_BLOCK + 1, last + 1):
-                z = z_of[m]
-                nc.scalar.activation(out=z[:], in_=z[:], func=FUNC.Ln)
-                nc.scalar.dma_start(out=out_items[items[m][1], items[m][2]], in_=z[:])
+            def table_quarter(k):
+                for entry in quarters[k]:
+                    entry[0](entry[1], entry[2])
+                sum_squares(s + 3, k)
 
-        for s in range(-4, len(items) + 2):
-            keep_rows(s)
-            load(s + 4)
-            transpose(s + 2)
+            spread_g(s)
+            numerator(s, 0)
+            multiply(s, 2)
+            numerator(s, 1)
+            multiply(s, 3)
+            factors(s + 1, 0)
+            regroup(s + 2, 0)
+            transpose(s + 2, 2)
+            table_quarter(0)
+            numerator(s, 2)
+            factors(s + 1, 1)
+            numerator(s, 3)
+            regroup(s + 2, 1)
+            transpose(s + 2, 3)
+            table_quarter(1)
+            cosh(s, 0)
+            factors(s + 1, 2)
+            cosh(s, 1)
+            cosh(s, 2)
+            factors(s + 1, 3)
+            cosh(s, 3)
+            table_quarter(2)
+            spread_sums(s + 1)
             quantise(s + 1)
-            row_factors(s + 1)
-            numerator(s)
-            multiply(s + 1)
-            square_root(s - 1)
-            sum_squares(s + 3)
-            regroup(s + 2)
-            spread_over_partitions(s + 1)
-            cosh_clipped(s)
-            add_root(s - 2)
-            logarithms(s - 2)
+            multiply(s + 1, 0)
+            multiply(s + 1, 1)
+            regroup(s + 2, 2)
+            transpose(s + 3, 0)
+            regroup(s + 2, 3)
+            transpose(s + 3, 1)
+            keep_a_row(s + 1)
+            table_quarter(3)
+        assert done == len(table_work)

@@ -281,10 +281,10 @@ def tile_hyperbolicdistancelayer_t_kernel(tc, x, y, out):
             nc.gpsimd.tensor_scalar(
                 out=z_of[m][:, cols],
                 in0=z_of[m][:, cols],
-                scalar1=1.0,
-                scalar2=COSH_MAX,
-                op0=ALU.max,
-                op1=ALU.min,
+                scalar1=COSH_MAX,
+                scalar2=1.0,
+                op0=ALU.min,
+                op1=ALU.max,
             )
 
         def square(m, half):

@@ -28,11 +28,15 @@ COSH_MAX = (1.0 + NORM_MAX * NORM_MAX) / (1.0 - NORM_MAX * NORM_MAX)
 OUTSIDE = 1024.0
 TINY = 1e-30
 
-LOG_BLOCKS = (2, 4, 4, 4, 2)
+LOG_BLOCKS = (2, 4, 5, 5)
+AHEAD = 5
+BUD = 6
 LAG = 2
-BUD = 24
-BUD2 = 48
-LNC = 4
+SLOTS = 4
+RG_S = ()
+GP = 512
+QH = 1
+LATE = (17,)
 
 
 def tile_hyperbolicdistancelayer_t_kernel(tc, x, y, out):
@@ -48,29 +52,29 @@ def tile_hyperbolicdistancelayer_t_kernel(tc, x, y, out):
         for g in range(GROUPS):
             items.append(("x", b, g))
     x_order = [m for m in range(len(items)) if items[m][0] == "x"]
+    last = x_order[-1]
 
     table_work = []
     first = 0
     for size in LOG_BLOCKS:
         block = list(range(first, first + size))
         first += size
-        table_work.extend(("sqrt", n, half) for n in block for half in range(2))
-        table_work.extend(("ln", n, t) for n in block for t in range(TILES))
+        table_work.extend(("root", n, half) for n in block for half in range(2))
+        table_work.extend(("ln", n, half) for n in block for half in range(2))
 
     with (
         tc.tile_pool(name="const", bufs=1) as const,
-        tc.tile_pool(name="raw_pool", bufs=4) as raw_pool,
+        tc.tile_pool(name="raw_pool", bufs=7) as raw_pool,
         tc.tile_pool(name="grouped_pool", bufs=2) as grouped_pool,
         tc.tile_pool(name="mx_pool", bufs=2) as mx_pool,
-        tc.tile_pool(name="small", bufs=4) as small,
+        tc.tile_pool(name="small", bufs=8) as small,
+        tc.tile_pool(name="diag_pool", bufs=2) as diag_pool,
         tc.tile_pool(name="rows_pool", bufs=2) as rows_pool,
-        tc.tile_pool(name="z_pool", bufs=9) as z_pool,
-        tc.tile_pool(name="root_pool", bufs=8) as root_pool,
-        tc.tile_pool(name="out_pool", bufs=2) as out_pool,
-        tc.psum_pool(name="turned_pool", bufs=2) as turned_pool,
-        tc.psum_pool(name="dot_pool", bufs=2) as dot_pool,
-        tc.psum_pool(name="spread_pool", bufs=1) as spread_pool,
-        tc.psum_pool(name="sum_pool", bufs=3) as sum_pool,
+        tc.tile_pool(name="z_pool", bufs=11) as z_pool,
+        tc.tile_pool(name="root_pool", bufs=4) as root_pool,
+        tc.psum_pool(name="turned_pool", bufs=3) as turned_pool,
+        tc.psum_pool(name="dot_pool", bufs=4) as dot_pool,
+        tc.psum_pool(name="g_pool", bufs=1) as g_pool,
         tc.manual_schedule(),
     ):
         identity = const.tile([P, P], F32)
@@ -79,8 +83,10 @@ def tile_hyperbolicdistancelayer_t_kernel(tc, x, y, out):
         nc.vector.memset(minus_one[:], -1.0)
         squares = const.tile([P, TILES * D], BF16)
 
+        gram_tiles = {m: (2, 3) if m % 2 else (3,) for m in range(18) if m % 9}
         raw = {}
         sumsq = {}
+        gram_bank = {}
         turned = {}
         grouped = {}
         codes = {}
@@ -94,7 +100,6 @@ def tile_hyperbolicdistancelayer_t_kernel(tc, x, y, out):
         dots = {}
         z_of = {}
         root = {}
-        out_of = {}
         y_of = {}
 
         def kind(m):
@@ -106,19 +111,51 @@ def tile_hyperbolicdistancelayer_t_kernel(tc, x, y, out):
             what, b, g = items[m]
             rows = raw_pool.tile([P, TILES * D], BF16)
             raw[m] = rows
+            sums = small.tile([P, TILES], F32)
+            sumsq[m] = sums
             if what == "x":
                 nc.sync.dma_start(out=rows[:], in_=x_items[b, g])
             else:
-                nc.sync.dma_start(
-                    out=rows[:].rearrange("p (t k) -> p t k", t=TILES), in_=y_items[b]
+                nc.sync.dma_start(out=rows[:].rearrange("p (t k) -> p t k", t=TILES), in_=y_items[b])
+
+        def by_gram(m):
+            return gram_tiles.get(m, ())
+
+        def gram(m):
+            if not by_gram(m):
+                return
+            bank = turned_pool.tile([P, PASSES, HALVES, P], F32)
+            gram_bank[m] = bank[:].rearrange("p c u r -> p (c u) r")
+            order = "q (c t r e) -> q c t r e" if kind(m) == "y" else "q (t c r e) -> q c t r e"
+            values = grouped[m][:].rearrange(order, c=PASSES, t=TILES, r=P)
+            for n, t in enumerate(by_gram(m)):
+                for c in range(PASSES):
+                    for e in range(4):
+                        block = values[:, c, t, :, e]
+                        nc.tensor.matmul(
+                            out=gram_bank[m][:, n, :],
+                            lhsT=block,
+                            rhs=block,
+                            start=(c == 0 and e == 0),
+                            stop=(c == PASSES - 1 and e == 3),
+                        )
+
+        def diagonal(m):
+            for n, t in enumerate(by_gram(m)):
+                off = diag_pool.tile([P, P], F32)
+                nc.vector.scalar_tensor_tensor(
+                    out=off[:],
+                    in0=gram_bank[m][:, n, :],
+                    scalar=1.0,
+                    in1=identity[:],
+                    op0=ALU.mult,
+                    op1=ALU.mult,
+                    accum_out=sumsq[m][:, t : t + 1],
                 )
 
         def sum_squares(m, t):
-            if kind(m) == "none":
+            if kind(m) == "none" or t in by_gram(m):
                 return
-            if t == 0:
-                sums = small.tile([P, TILES], F32)
-                sumsq[m] = sums
             cols = slice(t * D, (t + 1) * D)
             nc.scalar.activation(
                 out=squares[:, cols],
@@ -144,50 +181,56 @@ def tile_hyperbolicdistancelayer_t_kernel(tc, x, y, out):
             if t == 0:
                 values = grouped_pool.tile([P, TILES * D], BF16, align_bytes=64)
                 grouped[m] = values
-            order = "q (t c r u) -> q t c r u" if kind(m) == "y" else "q (c t r u) -> q t c r u"
+            order = "q (t c r u) -> q t c r u" if kind(m) == "x" else "q (c t r u) -> q t c r u"
             places = grouped[m][:].bitcast(F32).rearrange(order, t=TILES, c=PASSES, r=P, u=HALVES)
-            nc.vector.tensor_copy(
-                out=places[:, t], in_=turned[m, t][:].rearrange("q c u r -> q c r u")
-            )
+            copy = nc.scalar.copy if (kind(m) == "x" and t in RG_S) else nc.vector.tensor_copy
+            copy(out=places[:, t], in_=turned[m, t][:].rearrange("q c u r -> q c r u"))
 
-        def quantise(m):
+        def quantise(m, half):
             if kind(m) == "none":
                 return
             tag = kind(m)
-            packed = mx_pool.tile([P, TILES * D // 4], U32, align_bytes=64, tag=tag + "_codes")
-            plane = mx_pool.tile([P, TILES * D // 4], U8, align_bytes=64, tag=tag + "_scales")
-            codes[m] = packed
-            scales[m] = plane
-            nc.vector.quantize_mx(out=packed[:].bitcast(FP8X4), scales=plane[:], in_=grouped[m][:])
+            if half == 0:
+                packed = mx_pool.tile([P, TILES * D // 4], U32, align_bytes=64, tag=tag + "_codes")
+                plane = mx_pool.tile([P, TILES * D // 4], U8, align_bytes=64, tag=tag + "_scales")
+                codes[m] = packed
+                scales[m] = plane
+            if QH == 1 and half == 1:
+                return
+            w = TILES * D // QH
+            cols = slice(half * w // 4, (half + 1) * w // 4)
+            nc.vector.quantize_mx(
+                out=codes[m][:, cols].bitcast(FP8X4),
+                scales=scales[m][:, cols],
+                in_=grouped[m][:, half * w : (half + 1) * w],
+            )
 
         def factors(m, stage):
             if kind(m) == "none":
                 return
             v = sumsq[m]
             if stage == 0:
+                a = small.tile([P, TILES], F32, tag=kind(m) + "_a")
                 h = small.tile([P, TILES], F32)
                 h_out = small.tile([P, TILES], F32)
+                a_of[m] = a
                 h_of[m] = (h, h_out)
                 nc.vector.tensor_scalar(
                     out=h[:], in0=v[:], scalar1=-0.5, scalar2=0.5, op0=ALU.mult, op1=ALU.add
                 )
-                if kind(m) == "y":
-                    a = small.tile([P, TILES], F32, tag="y_a")
-                    a_of[m] = a
-                    nc.vector.tensor_scalar(
-                        out=a[:], in0=v[:], scalar1=0.5, scalar2=0.5, op0=ALU.mult, op1=ALU.add
-                    )
-            elif stage == 1:
                 nc.vector.tensor_scalar(
-                    out=h_of[m][1][:],
+                    out=h_out[:],
                     in0=v[:],
                     scalar1=0.5 / OUTSIDE,
                     scalar2=-0.5 / OUTSIDE,
                     op0=ALU.mult,
                     op1=ALU.add,
                 )
-            elif stage == 2:
+            elif stage == 1:
                 h, h_out = h_of[m]
+                nc.vector.tensor_scalar(
+                    out=a_of[m][:], in0=v[:], scalar1=0.5, scalar2=0.5, op0=ALU.mult, op1=ALU.add
+                )
                 nc.vector.scalar_tensor_tensor(
                     out=h[:], in0=h_out[:], scalar=TINY, in1=h[:], op0=ALU.max, op1=ALU.max
                 )
@@ -195,11 +238,8 @@ def tile_hyperbolicdistancelayer_t_kernel(tc, x, y, out):
                 g = small.tile([P, TILES], F32, tag=kind(m) + "_g")
                 g_of[m] = g
                 nc.vector.reciprocal(out=g[:], in_=h_of[m][0][:])
-                if kind(m) == "y":
-                    y_of[items[m][1]] = m
 
-        def spread(m, column, tag):
-            bank = spread_pool.tile([P, ITEM_ROWS], F32)
+        def spread(bank, column):
             for t in range(TILES):
                 nc.tensor.transpose(
                     bank[:, t * P : (t + 1) * P],
@@ -208,77 +248,75 @@ def tile_hyperbolicdistancelayer_t_kernel(tc, x, y, out):
                 )
             return bank
 
-        def spread_sums(m):
-            if kind(m) == "x":
-                a_bank[m] = spread(m, sumsq[m], "a_bank")
+        def spread_rows(m):
+            if kind(m) != "y":
+                return
+            acc = dot_pool.tile([P, M], F32)
+            a_bank[m] = spread(acc[:], a_of[m])
+            g_row = g_pool.tile([P, M], F32)
+            g_bank[m] = spread(g_row[:], g_of[m])
 
         def keep_a_row(m):
-            if kind(m) != "x":
+            if kind(m) != "y":
                 return
-            row = rows_pool.tile([P, ITEM_ROWS], F32)
+            row = rows_pool.tile([P, M], F32)
             a_row[m] = row
-            nc.vector.tensor_scalar(
-                out=row[:], in0=a_bank[m][:], scalar1=0.5, scalar2=0.5, op0=ALU.mult, op1=ALU.add
-            )
+            nc.vector.tensor_copy(out=row[:], in_=a_bank[m])
+            y_of[items[m][1]] = m
 
-        def spread_g(m):
-            if kind(m) == "x":
-                g_bank[m] = spread(m, g_of[m], "g_bank")
-
-        def multiply(m, j):
+        def multiply(m, t):
             if kind(m) != "x":
                 return
-            ym = y_of[items[m][1]]
-            acc = dot_pool.tile([P, ITEM_ROWS], F32)
-            dots[m, j] = acc
+            ym = codes_of_y[items[m][1]]
+            acc = dot_pool.tile([P, M], F32)
+            dots[m, t] = acc
             for c in range(PASSES):
-                y_cols = slice((j * PASSES + c) * P, (j * PASSES + c + 1) * P)
-                x_cols = slice(c * ITEM_ROWS, (c + 1) * ITEM_ROWS)
+                x_cols = slice((t * PASSES + c) * P, (t * PASSES + c + 1) * P)
+                y_cols = slice(c * M, (c + 1) * M)
                 nc.tensor.matmul_mx(
                     out=acc[:],
-                    lhsT=codes[ym][:, y_cols].bitcast(FP8X4),
-                    lhsT_scale=scales[ym][:, y_cols],
-                    rhs=codes[m][:, x_cols].bitcast(FP8X4),
-                    rhs_scale=scales[m][:, x_cols],
+                    lhsT=codes[m][:, x_cols].bitcast(FP8X4),
+                    lhsT_scale=scales[m][:, x_cols],
+                    rhs=codes[ym][:, y_cols].bitcast(FP8X4),
+                    rhs_scale=scales[ym][:, y_cols],
                     start=(c == 0),
                     stop=(c == PASSES - 1),
                 )
 
-        def numerator(m, j):
+        codes_of_y = {items[m][1]: m for m in range(len(items)) if items[m][0] == "y"}
+
+        def numerator(m, t):
             if kind(m) != "x":
                 return
             ym = y_of[items[m][1]]
-            if j == 0:
+            if t == 0:
                 z = z_pool.tile([P, OUT_COLS], F32)
                 z_of[m] = z
             nc.vector.scalar_tensor_tensor(
-                out=z_of[m][:, j * ITEM_ROWS : (j + 1) * ITEM_ROWS],
-                in0=a_row[m][:],
-                scalar=a_of[ym][:, j : j + 1],
-                in1=dots[m, j][:],
+                out=z_of[m][:, t * M : (t + 1) * M],
+                in0=a_row[ym][:],
+                scalar=a_of[m][:, t : t + 1],
+                in1=dots[m, t][:],
                 op0=ALU.mult,
                 op1=ALU.subtract,
             )
 
-        def cosh(m, j):
+        def cosh(m, t):
             if kind(m) != "x":
                 return
             ym = y_of[items[m][1]]
-            cols = slice(j * ITEM_ROWS, (j + 1) * ITEM_ROWS)
+            cols = slice(t * M, (t + 1) * M)
             nc.vector.scalar_tensor_tensor(
                 out=z_of[m][:, cols],
                 in0=z_of[m][:, cols],
-                scalar=g_of[ym][:, j : j + 1],
-                in1=g_bank[m][:],
+                scalar=g_of[m][:, t : t + 1],
+                in1=g_bank[ym],
                 op0=ALU.mult,
                 op1=ALU.mult,
             )
 
-        def clip(m, half):
-            if kind(m) != "x":
-                return
-            cols = slice(half * HALF, (half + 1) * HALF)
-            nc.gpsimd.tensor_scalar(
+        def clip(engine, m, cols):
+            engine.tensor_scalar(
                 out=z_of[m][:, cols],
                 in0=z_of[m][:, cols],
                 scalar1=COSH_MAX,
@@ -287,96 +325,100 @@ def tile_hyperbolicdistancelayer_t_kernel(tc, x, y, out):
                 op1=ALU.max,
             )
 
-        def square(m, half):
-            if kind(m) != "x":
-                return
-            if half == 0:
-                r = root_pool.tile([P, OUT_COLS], F32)
-                root[m] = r
-            cols = slice(half * HALF, (half + 1) * HALF)
-            nc.gpsimd.tensor_tensor(
-                out=root[m][:, cols], in0=z_of[m][:, cols], in1=z_of[m][:, cols], op=ALU.mult
-            )
+        def new_root(m):
+            r = root_pool.tile([P, OUT_COLS], F32)
+            root[m] = r
 
-        def square_root(m, half):
-            cols = slice(half * HALF, (half + 1) * HALF)
+        def square(m, cols):
+            nc.scalar.activation(out=root[m][:, cols], in_=z_of[m][:, cols], func=FUNC.Square)
+
+        def square_root(m, cols):
             nc.scalar.activation(
                 out=root[m][:, cols], in_=root[m][:, cols], func=FUNC.Sqrt, bias=minus_one[:, 0:1]
             )
 
-        def logarithm(m, t):
-            bank = sum_pool.tile([P, M], F32)
-            for j in range(TILES):
-                cols = slice(j * ITEM_ROWS + t * P, j * ITEM_ROWS + (t + 1) * P)
-                place = bank[:, j * P : (j + 1) * P]
-                nc.tensor.matmul(
-                    place, lhsT=z_of[m][:, cols], rhs=identity[:], is_transpose=True, start=True, stop=False
-                )
-                nc.tensor.matmul(
-                    place, lhsT=root[m][:, cols], rhs=identity[:], is_transpose=True, start=False, stop=True
-                )
-            if t == 0:
-                result = out_pool.tile([P, OUT_COLS], F32)
-                out_of[m] = result
-            nc.scalar.activation(
-                out=out_of[m][:, t * M : (t + 1) * M], in_=bank[:], func=FUNC.Ln
+        def add_root(engine, m, cols):
+            engine.tensor_tensor(
+                out=z_of[m][:, cols], in0=z_of[m][:, cols], in1=root[m][:, cols], op=ALU.add
             )
-            if t == TILES - 1:
-                nc.scalar.dma_start(out=out_items[items[m][1], items[m][2]], in_=out_of[m][:])
+
+        def logarithm(m, cols):
+            nc.scalar.activation(out=z_of[m][:, cols], in_=z_of[m][:, cols], func=FUNC.Ln)
+
+        def store(m, cols):
+            nc.scalar.dma_start(out=out_items[items[m][1], items[m][2]][:, cols], in_=z_of[m][:, cols])
+
+        halves = (slice(0, HALF), slice(HALF, OUT_COLS))
+        everything = slice(0, OUT_COLS)
+
+        def pieces(half):
+            return [slice(a, a + GP) for a in range(half * HALF, (half + 1) * HALF, GP)]
 
         done = 0
-        for s in range(-5, len(items) + 6):
-            load(s + 5)
-            for half in range(2):
-                clip(s - 1, half)
-                square(s - 1, half)
-            squared = sum(1 for m in x_order if m <= s - LAG)
-            share = BUD if kind(s + 3) != "none" else BUD2
-            quarters = [[] for k in range(TILES)]
+        for s in range(-2 - AHEAD, len(items) + 6):
+            load(s + AHEAD + 2)
+            ready = sum(1 for m in x_order if m <= s - LAG or m == last and s >= last)
+            share = BUD if s < last else 1000
+            slots = [[] for k in range(SLOTS)]
             spent = 0
-            while spent < share and done < len(table_work) and table_work[done][1] < squared:
-                what, n, part = table_work[done]
-                m = x_order[n]
-                k = min(spent * TILES // share, TILES - 1)
-                quarters[k].append((square_root if what == "sqrt" else logarithm, m, part))
+            while spent < share and done < len(table_work) and table_work[done][1] < ready and (s > last or table_work[done][1] < len(x_order) - 1):
+                what, n, half = table_work[done]
+                slots[min(spent * SLOTS // share, SLOTS - 1)].append((what, x_order[n], half))
                 done += 1
-                spent += 3 if what == "sqrt" else LNC
+                spent += 2 if what == "root" else 1
 
-            def table_quarter(k):
-                for entry in quarters[k]:
-                    entry[0](entry[1], entry[2])
-                sum_squares(s + 3, k)
+            def table_slot(k):
+                for what, m, half in slots[k]:
+                    if what == "root":
+                        if half == 0:
+                            new_root(m)
+                        if m == last:
+                            for t in (2 * half, 2 * half + 1):
+                                cols = slice(t * M, (t + 1) * M)
+                                square(m, cols)
+                                square_root(m, cols)
+                                add_root(nc.vector, m, cols)
+                        else:
+                            square(m, halves[half])
+                            square_root(m, halves[half])
+                            for cols in pieces(half):
+                                add_root(nc.vector if m in LATE else nc.gpsimd, m, cols)
+                    elif m == last:
+                        for t in (2 * half, 2 * half + 1):
+                            logarithm(m, slice(t * M, (t + 1) * M))
+                            store(m, slice(t * M, (t + 1) * M))
+                    else:
+                        logarithm(m, halves[half])
+                        if half == 1:
+                            store(m, everything)
+                if k < TILES:
+                    sum_squares(s + AHEAD, k)
 
-            spread_g(s)
-            numerator(s, 0)
-            multiply(s, 2)
-            numerator(s, 1)
-            multiply(s, 3)
-            factors(s + 1, 0)
-            regroup(s + 2, 0)
-            transpose(s + 2, 2)
-            table_quarter(0)
-            numerator(s, 2)
+            if kind(s - 1) == "x" and s - 1 not in LATE:
+                for cols in pieces(0) + pieces(1):
+                    clip(nc.gpsimd, s - 1, cols)
+            for t in range(TILES):
+                numerator(s, t)
+                if t == 0:
+                    factors(s, 2)
+                if t % 2 == 1:
+                    quantise(s + 1, t // 2)
+            spread_rows(s)
+            keep_a_row(s)
+            for t in range(TILES):
+                multiply(s + 1, t)
+            for t in range(TILES):
+                regroup(s + 2, t)
+                transpose(s + 2, t + 2) if t < 2 else transpose(s + 3, t - 2)
+                cosh(s, t)
+                if t == 1:
+                    diagonal(s + 1)
+                elif t == 2:
+                    factors(s + 1, 0)
+                if s in LATE:
+                    cols = slice(t * M, (t + 1) * M)
+                    clip(nc.vector, s, cols)
+                table_slot(t)
             factors(s + 1, 1)
-            numerator(s, 3)
-            regroup(s + 2, 1)
-            transpose(s + 2, 3)
-            table_quarter(1)
-            cosh(s, 0)
-            factors(s + 1, 2)
-            cosh(s, 1)
-            cosh(s, 2)
-            factors(s + 1, 3)
-            cosh(s, 3)
-            table_quarter(2)
-            spread_sums(s + 1)
-            quantise(s + 1)
-            multiply(s + 1, 0)
-            multiply(s + 1, 1)
-            regroup(s + 2, 2)
-            transpose(s + 3, 0)
-            regroup(s + 2, 3)
-            transpose(s + 3, 1)
-            keep_a_row(s + 1)
-            table_quarter(3)
+            gram(s + 2)
         assert done == len(table_work)

@@ -25,10 +25,10 @@ HALF = OUT_COLS // 2
 
 NORM_MAX = 0.99
 COSH_MAX = (1.0 + NORM_MAX * NORM_MAX) / (1.0 - NORM_MAX * NORM_MAX)
-OUTSIDE = 1024.0
-TINY = 1e-30
+FLOOR = 1e-15
+ROOT_HALF = 0.5**0.5
 
-LOG_BLOCKS = (2, 4, 5, 5)
+LOG_BLOCKS = (3, 4, 5, 4)
 AHEAD = 5
 BUD = 6
 LAG = 2
@@ -37,6 +37,8 @@ RG_S = ()
 GP = 512
 QH = 1
 LATE = (17,)
+SPLIT = 1
+V_SUMS = ()
 
 
 def tile_hyperbolicdistancelayer_t_kernel(tc, x, y, out):
@@ -59,7 +61,7 @@ def tile_hyperbolicdistancelayer_t_kernel(tc, x, y, out):
     for size in LOG_BLOCKS:
         block = list(range(first, first + size))
         first += size
-        table_work.extend(("root", n, half) for n in block for half in range(2))
+        table_work.extend(("root", n, 0) for n in block)
         table_work.extend(("ln", n, half) for n in block for half in range(2))
 
     with (
@@ -81,6 +83,8 @@ def tile_hyperbolicdistancelayer_t_kernel(tc, x, y, out):
         make_identity(nc, identity[:])
         minus_one = const.tile([P, 1], F32)
         nc.vector.memset(minus_one[:], -1.0)
+        one = const.tile([P, 1], F32)
+        nc.vector.memset(one[:], 1.0)
         squares = const.tile([P, TILES * D], BF16)
 
         gram_tiles = {m: (2, 3) if m % 2 else (3,) for m in range(18) if m % 9}
@@ -91,7 +95,6 @@ def tile_hyperbolicdistancelayer_t_kernel(tc, x, y, out):
         grouped = {}
         codes = {}
         scales = {}
-        a_of = {}
         h_of = {}
         g_of = {}
         a_row = {}
@@ -113,7 +116,12 @@ def tile_hyperbolicdistancelayer_t_kernel(tc, x, y, out):
             raw[m] = rows
             sums = small.tile([P, TILES], F32)
             sumsq[m] = sums
-            if what == "x":
+            if m < SPLIT:
+                for t in range(TILES):
+                    cols = slice(t * D, (t + 1) * D)
+                    source = x_items[b, g][:, cols] if what == "x" else y_items[b][:, t]
+                    nc.sync.dma_start(out=rows[:, cols], in_=source)
+            elif what == "x":
                 nc.sync.dma_start(out=rows[:], in_=x_items[b, g])
             else:
                 nc.sync.dma_start(out=rows[:].rearrange("p (t k) -> p t k", t=TILES), in_=y_items[b])
@@ -146,7 +154,7 @@ def tile_hyperbolicdistancelayer_t_kernel(tc, x, y, out):
                 nc.vector.scalar_tensor_tensor(
                     out=off[:],
                     in0=gram_bank[m][:, n, :],
-                    scalar=1.0,
+                    scalar=0.5,
                     in1=identity[:],
                     op0=ALU.mult,
                     op1=ALU.mult,
@@ -157,12 +165,30 @@ def tile_hyperbolicdistancelayer_t_kernel(tc, x, y, out):
             if kind(m) == "none" or t in by_gram(m):
                 return
             cols = slice(t * D, (t + 1) * D)
+            if (m, t) in V_SUMS:
+                return
             nc.scalar.activation(
                 out=squares[:, cols],
                 in_=raw[m][:, cols],
                 func=FUNC.Square,
+                scale=ROOT_HALF,
                 accum_out=sumsq[m][:, t : t + 1],
             )
+
+        def sum_squares_on_vector(m):
+            for t in range(TILES):
+                if (m, t) in V_SUMS:
+                    cols = slice(t * D, (t + 1) * D)
+                    off = diag_pool.tile([P, D], BF16, tag="v_squares")
+                    nc.vector.scalar_tensor_tensor(
+                        out=off[:],
+                        in0=raw[m][:, cols],
+                        scalar=0.5,
+                        in1=raw[m][:, cols],
+                        op0=ALU.mult,
+                        op1=ALU.mult,
+                        accum_out=sumsq[m][:, t : t + 1],
+                    )
 
         def transpose(m, t):
             if kind(m) == "none":
@@ -208,36 +234,16 @@ def tile_hyperbolicdistancelayer_t_kernel(tc, x, y, out):
         def factors(m, stage):
             if kind(m) == "none":
                 return
-            v = sumsq[m]
             if stage == 0:
-                a = small.tile([P, TILES], F32, tag=kind(m) + "_a")
                 h = small.tile([P, TILES], F32)
-                h_out = small.tile([P, TILES], F32)
-                a_of[m] = a
-                h_of[m] = (h, h_out)
+                h_of[m] = h
                 nc.vector.tensor_scalar(
-                    out=h[:], in0=v[:], scalar1=-0.5, scalar2=0.5, op0=ALU.mult, op1=ALU.add
+                    out=h[:], in0=sumsq[m][:], scalar1=0.5, scalar2=-FLOOR, op0=ALU.subtract, op1=ALU.min
                 )
-                nc.vector.tensor_scalar(
-                    out=h_out[:],
-                    in0=v[:],
-                    scalar1=0.5 / OUTSIDE,
-                    scalar2=-0.5 / OUTSIDE,
-                    op0=ALU.mult,
-                    op1=ALU.add,
-                )
-            elif stage == 1:
-                h, h_out = h_of[m]
-                nc.vector.tensor_scalar(
-                    out=a_of[m][:], in0=v[:], scalar1=0.5, scalar2=0.5, op0=ALU.mult, op1=ALU.add
-                )
-                nc.vector.scalar_tensor_tensor(
-                    out=h[:], in0=h_out[:], scalar=TINY, in1=h[:], op0=ALU.max, op1=ALU.max
-                )
-            else:
+            elif stage == 2:
                 g = small.tile([P, TILES], F32, tag=kind(m) + "_g")
                 g_of[m] = g
-                nc.vector.reciprocal(out=g[:], in_=h_of[m][0][:])
+                nc.vector.reciprocal(out=g[:], in_=h_of[m][:])
 
         def spread(bank, column):
             for t in range(TILES):
@@ -252,7 +258,7 @@ def tile_hyperbolicdistancelayer_t_kernel(tc, x, y, out):
             if kind(m) != "y":
                 return
             acc = dot_pool.tile([P, M], F32)
-            a_bank[m] = spread(acc[:], a_of[m])
+            a_bank[m] = spread(acc[:], sumsq[m])
             g_row = g_pool.tile([P, M], F32)
             g_bank[m] = spread(g_row[:], g_of[m])
 
@@ -295,9 +301,9 @@ def tile_hyperbolicdistancelayer_t_kernel(tc, x, y, out):
             nc.vector.scalar_tensor_tensor(
                 out=z_of[m][:, t * M : (t + 1) * M],
                 in0=a_row[ym][:],
-                scalar=a_of[m][:, t : t + 1],
+                scalar=sumsq[m][:, t : t + 1],
                 in1=dots[m, t][:],
-                op0=ALU.mult,
+                op0=ALU.add,
                 op1=ALU.subtract,
             )
 
@@ -319,8 +325,8 @@ def tile_hyperbolicdistancelayer_t_kernel(tc, x, y, out):
             engine.tensor_scalar(
                 out=z_of[m][:, cols],
                 in0=z_of[m][:, cols],
-                scalar1=COSH_MAX,
-                scalar2=1.0,
+                scalar1=COSH_MAX - 1.0,
+                scalar2=0.0,
                 op0=ALU.min,
                 op1=ALU.max,
             )
@@ -330,7 +336,7 @@ def tile_hyperbolicdistancelayer_t_kernel(tc, x, y, out):
             root[m] = r
 
         def square(m, cols):
-            nc.scalar.activation(out=root[m][:, cols], in_=z_of[m][:, cols], func=FUNC.Square)
+            nc.scalar.activation(out=root[m][:, cols], in_=z_of[m][:, cols], func=FUNC.Square, bias=one[:, 0:1])
 
         def square_root(m, cols):
             nc.scalar.activation(
@@ -343,16 +349,16 @@ def tile_hyperbolicdistancelayer_t_kernel(tc, x, y, out):
             )
 
         def logarithm(m, cols):
-            nc.scalar.activation(out=z_of[m][:, cols], in_=z_of[m][:, cols], func=FUNC.Ln)
+            nc.scalar.activation(out=z_of[m][:, cols], in_=z_of[m][:, cols], func=FUNC.Ln, bias=one[:, 0:1])
 
         def store(m, cols):
             nc.scalar.dma_start(out=out_items[items[m][1], items[m][2]][:, cols], in_=z_of[m][:, cols])
 
-        halves = (slice(0, HALF), slice(HALF, OUT_COLS))
+        halves = [slice(0, HALF), slice(HALF, OUT_COLS)]
         everything = slice(0, OUT_COLS)
 
-        def pieces(half):
-            return [slice(a, a + GP) for a in range(half * HALF, (half + 1) * HALF, GP)]
+        def pieces(cols):
+            return [slice(a, a + GP) for a in range(cols.start, cols.stop, GP)]
 
         done = 0
         for s in range(-2 - AHEAD, len(items) + 6):
@@ -365,24 +371,24 @@ def tile_hyperbolicdistancelayer_t_kernel(tc, x, y, out):
                 what, n, half = table_work[done]
                 slots[min(spent * SLOTS // share, SLOTS - 1)].append((what, x_order[n], half))
                 done += 1
-                spent += 2 if what == "root" else 1
+                spent += 4 if what == "root" else 1
 
             def table_slot(k):
                 for what, m, half in slots[k]:
                     if what == "root":
-                        if half == 0:
-                            new_root(m)
-                        if m == last:
-                            for t in (2 * half, 2 * half + 1):
-                                cols = slice(t * M, (t + 1) * M)
-                                square(m, cols)
-                                square_root(m, cols)
-                                add_root(nc.vector, m, cols)
-                        else:
-                            square(m, halves[half])
-                            square_root(m, halves[half])
-                            for cols in pieces(half):
-                                add_root(nc.vector if m in LATE else nc.gpsimd, m, cols)
+                        new_root(m)
+                        quarters = [slice(t * M, (t + 1) * M) for t in range(TILES)]
+                        parts = quarters if m == last else halves
+                        square(m, parts[0])
+                        for now, ahead in zip(parts, parts[1:] + parts[:1]):
+                            if ahead != parts[0]:
+                                square(m, ahead)
+                            square_root(m, now)
+                            if m in LATE:
+                                add_root(nc.vector, m, now)
+                            else:
+                                for cols in pieces(now):
+                                    add_root(nc.gpsimd, m, cols)
                     elif m == last:
                         for t in (2 * half, 2 * half + 1):
                             logarithm(m, slice(t * M, (t + 1) * M))
@@ -395,7 +401,7 @@ def tile_hyperbolicdistancelayer_t_kernel(tc, x, y, out):
                     sum_squares(s + AHEAD, k)
 
             if kind(s - 1) == "x" and s - 1 not in LATE:
-                for cols in pieces(0) + pieces(1):
+                for cols in pieces(everything):
                     clip(nc.gpsimd, s - 1, cols)
             for t in range(TILES):
                 numerator(s, t)
@@ -403,6 +409,7 @@ def tile_hyperbolicdistancelayer_t_kernel(tc, x, y, out):
                     factors(s, 2)
                 if t % 2 == 1:
                     quantise(s + 1, t // 2)
+            sum_squares_on_vector(s + 2)
             spread_rows(s)
             keep_a_row(s)
             for t in range(TILES):
@@ -419,6 +426,5 @@ def tile_hyperbolicdistancelayer_t_kernel(tc, x, y, out):
                     cols = slice(t * M, (t + 1) * M)
                     clip(nc.vector, s, cols)
                 table_slot(t)
-            factors(s + 1, 1)
             gram(s + 2)
         assert done == len(table_work)

@@ -75,8 +75,9 @@ def tile_hyperbolicdistancelayer_t_kernel(tc, x, y, out):
         tc.tile_pool(name="z_pool", bufs=11) as z_pool,
         tc.tile_pool(name="root_pool", bufs=4) as root_pool,
         tc.psum_pool(name="turned_pool", bufs=3) as turned_pool,
-        tc.psum_pool(name="dot_pool", bufs=4) as dot_pool,
+        tc.psum_pool(name="dot_pool", bufs=3) as dot_pool,
         tc.psum_pool(name="g_pool", bufs=1) as g_pool,
+        tc.psum_pool(name="gram_pool", bufs=1) as gram_pool,
         tc.manual_schedule(),
     ):
         identity = const.tile([P, P], F32)
@@ -132,8 +133,8 @@ def tile_hyperbolicdistancelayer_t_kernel(tc, x, y, out):
         def gram(m):
             if not by_gram(m):
                 return
-            bank = turned_pool.tile([P, PASSES, HALVES, P], F32)
-            gram_bank[m] = bank[:].rearrange("p c u r -> p (c u) r")
+            products = gram_pool.tile([P, TILES, P], F32)
+            gram_bank[m] = products
             order = "q (c t r e) -> q c t r e" if kind(m) == "y" else "q (t c r e) -> q c t r e"
             values = grouped[m][:].rearrange(order, c=PASSES, t=TILES, r=P)
             for n, t in enumerate(by_gram(m)):
@@ -403,28 +404,33 @@ def tile_hyperbolicdistancelayer_t_kernel(tc, x, y, out):
             if kind(s - 1) == "x" and s - 1 not in LATE:
                 for cols in pieces(everything):
                     clip(nc.gpsimd, s - 1, cols)
-            for t in range(TILES):
-                numerator(s, t)
-                if t == 0:
-                    factors(s, 2)
-                if t % 2 == 1:
-                    quantise(s + 1, t // 2)
-            sum_squares_on_vector(s + 2)
+            quantise(s + 1, 0)
+            quantise(s + 1, 1)
+            diagonal(s)
+            transpose(s + 2, 2)
+            numerator(s, 0)
+            multiply(s, 3)
+            numerator(s, 1)
+            factors(s, 0)
+            numerator(s, 2)
+            factors(s, 2)
+            numerator(s, 3)
             spread_rows(s)
             keep_a_row(s)
-            for t in range(TILES):
-                multiply(s + 1, t)
+            multiply(s + 1, 0)
+            multiply(s + 1, 1)
             for t in range(TILES):
                 regroup(s + 2, t)
-                transpose(s + 2, t + 2) if t < 2 else transpose(s + 3, t - 2)
+                if t == 0:
+                    transpose(s + 2, 3)
+                    multiply(s + 1, 2)
+                elif t == 1:
+                    gram(s + 1)
+                else:
+                    transpose(s + 3, t - 2)
                 cosh(s, t)
-                if t == 1:
-                    diagonal(s + 1)
-                elif t == 2:
-                    factors(s + 1, 0)
                 if s in LATE:
                     cols = slice(t * M, (t + 1) * M)
                     clip(nc.vector, s, cols)
                 table_slot(t)
-            gram(s + 2)
         assert done == len(table_work)

@@ -28,17 +28,19 @@ COSH_MAX = (1.0 + NORM_MAX * NORM_MAX) / (1.0 - NORM_MAX * NORM_MAX)
 FLOOR = 1e-15
 ROOT_HALF = 0.5**0.5
 
-LOG_BLOCKS = (3, 4, 5, 4)
+LOG_BLOCKS = (2, 4, 5, 5)
 AHEAD = 5
 BUD = 6
-LAG = 2
+LAG = 1
 SLOTS = 4
 RG_S = ()
-GP = 512
+GP = 1024
 QH = 1
 LATE = (17,)
 SPLIT = 1
 V_SUMS = ()
+FENCE = True
+ADDS = 2
 
 
 def tile_hyperbolicdistancelayer_t_kernel(tc, x, y, out):
@@ -74,8 +76,8 @@ def tile_hyperbolicdistancelayer_t_kernel(tc, x, y, out):
         tc.tile_pool(name="rows_pool", bufs=2) as rows_pool,
         tc.tile_pool(name="z_pool", bufs=11) as z_pool,
         tc.tile_pool(name="root_pool", bufs=4) as root_pool,
-        tc.psum_pool(name="turned_pool", bufs=3) as turned_pool,
-        tc.psum_pool(name="dot_pool", bufs=3) as dot_pool,
+        tc.psum_pool(name="turned_pool", bufs=2) as turned_pool,
+        tc.psum_pool(name="dot_pool", bufs=4) as dot_pool,
         tc.psum_pool(name="g_pool", bufs=1) as g_pool,
         tc.psum_pool(name="gram_pool", bufs=1) as gram_pool,
         tc.manual_schedule(),
@@ -86,7 +88,7 @@ def tile_hyperbolicdistancelayer_t_kernel(tc, x, y, out):
         nc.vector.memset(minus_one[:], -1.0)
         one = const.tile([P, 1], F32)
         nc.vector.memset(one[:], 1.0)
-        squares = const.tile([P, TILES * D], BF16)
+        squares = const.tile([P, 2 * D], BF16)
 
         gram_tiles = {m: (2, 3) if m % 2 else (3,) for m in range(18) if m % 9}
         raw = {}
@@ -169,7 +171,7 @@ def tile_hyperbolicdistancelayer_t_kernel(tc, x, y, out):
             if (m, t) in V_SUMS:
                 return
             nc.scalar.activation(
-                out=squares[:, cols],
+                out=squares[:, t % 2 * D : (t % 2 + 1) * D],
                 in_=raw[m][:, cols],
                 func=FUNC.Square,
                 scale=ROOT_HALF,
@@ -210,7 +212,7 @@ def tile_hyperbolicdistancelayer_t_kernel(tc, x, y, out):
                 grouped[m] = values
             order = "q (t c r u) -> q t c r u" if kind(m) == "x" else "q (c t r u) -> q t c r u"
             places = grouped[m][:].bitcast(F32).rearrange(order, t=TILES, c=PASSES, r=P, u=HALVES)
-            copy = nc.scalar.copy if (kind(m) == "x" and t in RG_S) else nc.vector.tensor_copy
+            copy = nc.scalar.copy if (m, t) in RG_S else nc.vector.tensor_copy
             copy(out=places[:, t], in_=turned[m, t][:].rearrange("q c u r -> q c r u"))
 
         def quantise(m, half):
@@ -362,6 +364,7 @@ def tile_hyperbolicdistancelayer_t_kernel(tc, x, y, out):
             return [slice(a, a + GP) for a in range(cols.start, cols.stop, GP)]
 
         done = 0
+        adds = []
         for s in range(-2 - AHEAD, len(items) + 6):
             load(s + AHEAD + 2)
             ready = sum(1 for m in x_order if m <= s - LAG or m == last and s >= last)
@@ -388,8 +391,7 @@ def tile_hyperbolicdistancelayer_t_kernel(tc, x, y, out):
                             if m in LATE:
                                 add_root(nc.vector, m, now)
                             else:
-                                for cols in pieces(now):
-                                    add_root(nc.gpsimd, m, cols)
+                                adds.append((m, now))
                     elif m == last:
                         for t in (2 * half, 2 * half + 1):
                             logarithm(m, slice(t * M, (t + 1) * M))
@@ -401,33 +403,36 @@ def tile_hyperbolicdistancelayer_t_kernel(tc, x, y, out):
                 if k < TILES:
                     sum_squares(s + AHEAD, k)
 
+            diagonal(s)
+            gram(s + 1)
+            quantise(s + 1, 0)
+            quantise(s + 1, 1)
+            factors(s, 0)
+            factors(s, 2)
+            if kind(s) != "none" and FENCE:
+                seen = small.tile([P, TILES], F32)
+                nc.gpsimd.tensor_copy(out=seen[:], in_=g_of[s][:])
             if kind(s - 1) == "x" and s - 1 not in LATE:
                 for cols in pieces(everything):
                     clip(nc.gpsimd, s - 1, cols)
-            quantise(s + 1, 0)
-            quantise(s + 1, 1)
-            diagonal(s)
-            transpose(s + 2, 2)
-            numerator(s, 0)
-            multiply(s, 3)
-            numerator(s, 1)
-            factors(s, 0)
-            numerator(s, 2)
-            factors(s, 2)
-            numerator(s, 3)
+            quota = ADDS if s < last else 100
+            while adds and quota > 0:
+                m, part = adds.pop(0)
+                for cols in pieces(part):
+                    add_root(nc.gpsimd, m, cols)
+                quota -= 1
             spread_rows(s)
             keep_a_row(s)
-            multiply(s + 1, 0)
-            multiply(s + 1, 1)
+            for t in range(TILES):
+                numerator(s, t)
             for t in range(TILES):
                 regroup(s + 2, t)
-                if t == 0:
-                    transpose(s + 2, 3)
-                    multiply(s + 1, 2)
-                elif t == 1:
-                    gram(s + 1)
+                if t < 2:
+                    transpose(s + 2, t + 2)
+                    multiply(s + 1, t)
                 else:
                     transpose(s + 3, t - 2)
+                    multiply(s + 1, t)
                 cosh(s, t)
                 if s in LATE:
                     cols = slice(t * M, (t + 1) * M)

@@ -28,7 +28,7 @@ COSH_MAX = (1.0 + NORM_MAX * NORM_MAX) / (1.0 - NORM_MAX * NORM_MAX)
 FLOOR = 1e-15
 ROOT_HALF = 0.5**0.5
 
-LOG_BLOCKS = (2, 4, 5, 5)
+LOG_BLOCKS = (3, 4, 5, 4)
 AHEAD = 5
 BUD = 6
 LAG = 1
@@ -36,11 +36,16 @@ SLOTS = 4
 RG_S = ()
 GP = 1024
 QH = 1
-LATE = (17,)
+LATE = (16, 17)
 SPLIT = 1
 V_SUMS = ()
 FENCE = True
 ADDS = 2
+FIRST = 3
+CV = 0
+CP = 1024
+BUD2 = 8
+KEEP = 1
 
 
 def tile_hyperbolicdistancelayer_t_kernel(tc, x, y, out):
@@ -90,7 +95,7 @@ def tile_hyperbolicdistancelayer_t_kernel(tc, x, y, out):
         nc.vector.memset(one[:], 1.0)
         squares = const.tile([P, 2 * D], BF16)
 
-        gram_tiles = {m: (2, 3) if m % 2 else (3,) for m in range(18) if m % 9}
+        gram_tiles = {m: (2, 3) if m % 4 else (3,) for m in range(18) if m % 9 > 1}
         raw = {}
         sumsq = {}
         gram_bank = {}
@@ -368,12 +373,16 @@ def tile_hyperbolicdistancelayer_t_kernel(tc, x, y, out):
         for s in range(-2 - AHEAD, len(items) + 6):
             load(s + AHEAD + 2)
             ready = sum(1 for m in x_order if m <= s - LAG or m == last and s >= last)
-            share = BUD if s < last else 1000
+            share = BUD if kind(s + AHEAD) != "none" else BUD2 if s < last else 1000
             slots = [[] for k in range(SLOTS)]
             spent = 0
             while spent < share and done < len(table_work) and table_work[done][1] < ready and (s > last or table_work[done][1] < len(x_order) - 1):
                 what, n, half = table_work[done]
-                slots[min(spent * SLOTS // share, SLOTS - 1)].append((what, x_order[n], half))
+                slot = min(spent * SLOTS // share, SLOTS - 1)
+                if what == "root" and x_order[n] == s - 1 and s <= last:
+                    slot = max(slot, FIRST)
+                slot = max([slot] + [k for k in range(SLOTS) if slots[k]])
+                slots[slot].append((what, x_order[n], half))
                 done += 1
                 spent += 4 if what == "root" else 1
 
@@ -404,17 +413,21 @@ def tile_hyperbolicdistancelayer_t_kernel(tc, x, y, out):
                     sum_squares(s + AHEAD, k)
 
             diagonal(s)
-            gram(s + 1)
+            if kind(s) != "y":
+                gram(s + 1)
+            numerator(s, 0)
+            factors(s, 0)
             quantise(s + 1, 0)
             quantise(s + 1, 1)
-            factors(s, 0)
             factors(s, 2)
+            if CV and kind(s - 1) == "x" and s - 1 not in LATE:
+                clip(nc.vector, s - 1, slice(OUT_COLS - CV, OUT_COLS))
             if kind(s) != "none" and FENCE:
                 seen = small.tile([P, TILES], F32)
                 nc.gpsimd.tensor_copy(out=seen[:], in_=g_of[s][:])
             if kind(s - 1) == "x" and s - 1 not in LATE:
-                for cols in pieces(everything):
-                    clip(nc.gpsimd, s - 1, cols)
+                for a in range(0, OUT_COLS - CV, CP):
+                    clip(nc.gpsimd, s - 1, slice(a, min(a + CP, OUT_COLS - CV)))
             quota = ADDS if s < last else 100
             while adds and quota > 0:
                 m, part = adds.pop(0)
@@ -422,8 +435,9 @@ def tile_hyperbolicdistancelayer_t_kernel(tc, x, y, out):
                     add_root(nc.gpsimd, m, cols)
                 quota -= 1
             spread_rows(s)
-            keep_a_row(s)
-            for t in range(TILES):
+            if kind(s) == "y":
+                gram(s + 1)
+            for t in range(1, TILES):
                 numerator(s, t)
             for t in range(TILES):
                 regroup(s + 2, t)
@@ -433,6 +447,8 @@ def tile_hyperbolicdistancelayer_t_kernel(tc, x, y, out):
                 else:
                     transpose(s + 3, t - 2)
                     multiply(s + 1, t)
+                if t == KEEP:
+                    keep_a_row(s)
                 cosh(s, t)
                 if s in LATE:
                     cols = slice(t * M, (t + 1) * M)

@@ -360,7 +360,7 @@ def tile_hyperbolicdistancelayer_t_kernel(tc, x, y, out):
             nc.scalar.activation(out=z_of[m][:, cols], in_=z_of[m][:, cols], func=FUNC.Ln, bias=one[:, 0:1])
 
         def store(m, cols):
-            nc.scalar.dma_start(out=out_items[items[m][1], items[m][2]][:, cols], in_=z_of[m][:, cols])
+            nc.sync.dma_start(out=out_items[items[m][1], items[m][2]][:, cols], in_=z_of[m][:, cols])
 
         halves = [slice(0, HALF), slice(HALF, OUT_COLS)]
         everything = slice(0, OUT_COLS)

@@ -28,7 +28,7 @@ COSH_MAX = (1.0 + NORM_MAX * NORM_MAX) / (1.0 - NORM_MAX * NORM_MAX)
 FLOOR = 1e-15
 ROOT_HALF = 0.5**0.5
 
-LOG_BLOCKS = (3, 4, 5, 4)
+LOG_BLOCKS = (3, 4, 4, 4, 1)
 AHEAD = 5
 BUD = 6
 LAG = 1
@@ -46,10 +46,18 @@ CV = 0
 CP = 1024
 BUD2 = 8
 KEEP = 1
+ADDLAG = 1
+ADDS_FIRST = False
+LAGGED = False
+SYNC_STORE = True
+GATE = True
+V_SQUARES = (17,)
+SQ_EARLY = False
 
 
 def tile_hyperbolicdistancelayer_t_kernel(tc, x, y, out):
     nc = tc.nc
+    STORE = nc.sync if SYNC_STORE else nc.scalar
 
     x_items = x.rearrange("b (g p t) k -> b g p (t k)", p=P, t=TILES)
     y_items = y.rearrange("b (t p) k -> b p t k", p=P)
@@ -65,11 +73,17 @@ def tile_hyperbolicdistancelayer_t_kernel(tc, x, y, out):
 
     table_work = []
     first = 0
+    rooted = []
     for size in LOG_BLOCKS:
         block = list(range(first, first + size))
         first += size
         table_work.extend(("root", n, 0) for n in block)
-        table_work.extend(("ln", n, half) for n in block for half in range(2))
+        if LAGGED:
+            table_work.extend(("ln", n, half) for n in rooted for half in range(2))
+            rooted = block
+        else:
+            table_work.extend(("ln", n, half) for n in block for half in range(2))
+    table_work.extend(("ln", n, half) for n in rooted for half in range(2))
 
     with (
         tc.tile_pool(name="const", bufs=1) as const,
@@ -183,20 +197,20 @@ def tile_hyperbolicdistancelayer_t_kernel(tc, x, y, out):
                 accum_out=sumsq[m][:, t : t + 1],
             )
 
-        def sum_squares_on_vector(m):
-            for t in range(TILES):
-                if (m, t) in V_SUMS:
-                    cols = slice(t * D, (t + 1) * D)
-                    off = diag_pool.tile([P, D], BF16, tag="v_squares")
-                    nc.vector.scalar_tensor_tensor(
-                        out=off[:],
-                        in0=raw[m][:, cols],
-                        scalar=0.5,
-                        in1=raw[m][:, cols],
-                        op0=ALU.mult,
-                        op1=ALU.mult,
-                        accum_out=sumsq[m][:, t : t + 1],
-                    )
+        def sum_squares_on_vector(m, t):
+            if (m, t) not in V_SUMS:
+                return
+            cols = slice(t * D, (t + 1) * D)
+            off = diag_pool.tile([P, D], BF16, tag="v_squares")
+            nc.vector.scalar_tensor_tensor(
+                out=off[:],
+                in0=raw[m][:, cols],
+                scalar=0.5,
+                in1=raw[m][:, cols],
+                op0=ALU.mult,
+                op1=ALU.mult,
+                accum_out=sumsq[m][:, t : t + 1],
+            )
 
         def transpose(m, t):
             if kind(m) == "none":
@@ -346,6 +360,16 @@ def tile_hyperbolicdistancelayer_t_kernel(tc, x, y, out):
         def square(m, cols):
             nc.scalar.activation(out=root[m][:, cols], in_=z_of[m][:, cols], func=FUNC.Square, bias=one[:, 0:1])
 
+        def square_on_vector(m, cols):
+            nc.vector.scalar_tensor_tensor(
+                out=root[m][:, cols],
+                in0=z_of[m][:, cols],
+                scalar=2.0,
+                in1=z_of[m][:, cols],
+                op0=ALU.add,
+                op1=ALU.mult,
+            )
+
         def square_root(m, cols):
             nc.scalar.activation(
                 out=root[m][:, cols], in_=root[m][:, cols], func=FUNC.Sqrt, bias=minus_one[:, 0:1]
@@ -360,7 +384,7 @@ def tile_hyperbolicdistancelayer_t_kernel(tc, x, y, out):
             nc.scalar.activation(out=z_of[m][:, cols], in_=z_of[m][:, cols], func=FUNC.Ln, bias=one[:, 0:1])
 
         def store(m, cols):
-            nc.sync.dma_start(out=out_items[items[m][1], items[m][2]][:, cols], in_=z_of[m][:, cols])
+            STORE.dma_start(out=out_items[items[m][1], items[m][2]][:, cols], in_=z_of[m][:, cols])
 
         halves = [slice(0, HALF), slice(HALF, OUT_COLS)]
         everything = slice(0, OUT_COLS)
@@ -369,49 +393,10 @@ def tile_hyperbolicdistancelayer_t_kernel(tc, x, y, out):
             return [slice(a, a + GP) for a in range(cols.start, cols.stop, GP)]
 
         done = 0
+        added = set(LATE)
         adds = []
         for s in range(-2 - AHEAD, len(items) + 6):
             load(s + AHEAD + 2)
-            ready = sum(1 for m in x_order if m <= s - LAG or m == last and s >= last)
-            share = BUD if kind(s + AHEAD) != "none" else BUD2 if s < last else 1000
-            slots = [[] for k in range(SLOTS)]
-            spent = 0
-            while spent < share and done < len(table_work) and table_work[done][1] < ready and (s > last or table_work[done][1] < len(x_order) - 1):
-                what, n, half = table_work[done]
-                slot = min(spent * SLOTS // share, SLOTS - 1)
-                if what == "root" and x_order[n] == s - 1 and s <= last:
-                    slot = max(slot, FIRST)
-                slot = max([slot] + [k for k in range(SLOTS) if slots[k]])
-                slots[slot].append((what, x_order[n], half))
-                done += 1
-                spent += 4 if what == "root" else 1
-
-            def table_slot(k):
-                for what, m, half in slots[k]:
-                    if what == "root":
-                        new_root(m)
-                        quarters = [slice(t * M, (t + 1) * M) for t in range(TILES)]
-                        parts = quarters if m == last else halves
-                        square(m, parts[0])
-                        for now, ahead in zip(parts, parts[1:] + parts[:1]):
-                            if ahead != parts[0]:
-                                square(m, ahead)
-                            square_root(m, now)
-                            if m in LATE:
-                                add_root(nc.vector, m, now)
-                            else:
-                                adds.append((m, now))
-                    elif m == last:
-                        for t in (2 * half, 2 * half + 1):
-                            logarithm(m, slice(t * M, (t + 1) * M))
-                            store(m, slice(t * M, (t + 1) * M))
-                    else:
-                        logarithm(m, halves[half])
-                        if half == 1:
-                            store(m, everything)
-                if k < TILES:
-                    sum_squares(s + AHEAD, k)
-
             diagonal(s)
             if kind(s) != "y":
                 gram(s + 1)
@@ -425,21 +410,84 @@ def tile_hyperbolicdistancelayer_t_kernel(tc, x, y, out):
             if kind(s) != "none" and FENCE:
                 seen = small.tile([P, TILES], F32)
                 nc.gpsimd.tensor_copy(out=seen[:], in_=g_of[s][:])
-            if kind(s - 1) == "x" and s - 1 not in LATE:
-                for a in range(0, OUT_COLS - CV, CP):
-                    clip(nc.gpsimd, s - 1, slice(a, min(a + CP, OUT_COLS - CV)))
+            if not ADDS_FIRST:
+                if kind(s - 1) == "x" and s - 1 not in LATE:
+                    for a in range(0, OUT_COLS - CV, CP):
+                        clip(nc.gpsimd, s - 1, slice(a, min(a + CP, OUT_COLS - CV)))
+            fresh = set()
             quota = ADDS if s < last else 100
-            while adds and quota > 0:
-                m, part = adds.pop(0)
+            while adds and quota > 0 and adds[0][2] <= s - ADDLAG:
+                m, part, when = adds.pop(0)
                 for cols in pieces(part):
                     add_root(nc.gpsimd, m, cols)
+                if part == halves[1]:
+                    added.add(m)
+                    fresh.add(m)
                 quota -= 1
+            if ADDS_FIRST:
+                if kind(s - 1) == "x" and s - 1 not in LATE:
+                    for a in range(0, OUT_COLS - CV, CP):
+                        clip(nc.gpsimd, s - 1, slice(a, min(a + CP, OUT_COLS - CV)))
+            ready = sum(1 for m in x_order if m <= s - LAG or m == last and s >= last)
+            share = BUD if kind(s + AHEAD) != "none" else BUD2 if s < last else 1000
+            slots = [[] for k in range(SLOTS)]
+            spent = 0
+            while spent < share and done < len(table_work) and table_work[done][1] < ready and (s > last or table_work[done][1] < len(x_order) - 1):
+                what, n, half = table_work[done]
+                if what == "ln" and GATE and x_order[n] not in added:
+                    break
+                slot = min(spent * SLOTS // share, SLOTS - 1)
+                if what == "root" and x_order[n] == s - 1 and s <= last or what == "ln" and x_order[n] in fresh:
+                    slot = max(slot, FIRST)
+                slot = max([slot] + [k for k in range(SLOTS) if slots[k]])
+                slots[slot].append((what, x_order[n], half))
+                done += 1
+                spent += 4 if what == "root" else 1
+
+            def table_slot(k):
+                for what, m, half in slots[k]:
+                    if what == "root":
+                        if not (SQ_EARLY and m == last):
+                            new_root(m)
+                        quarters = [slice(t * M, (t + 1) * M) for t in range(TILES)]
+                        parts = quarters if m == last else halves
+                        if m in V_SQUARES:
+                            if not (SQ_EARLY and m == last):
+                                for now in parts:
+                                    square_on_vector(m, now)
+                        else:
+                            square(m, parts[0])
+                        for now, ahead in zip(parts, parts[1:] + parts[:1]):
+                            if m in V_SQUARES:
+                                nc.scalar.activation(out=root[m][:, now], in_=root[m][:, now], func=FUNC.Sqrt)
+                            else:
+                                if ahead != parts[0]:
+                                    square(m, ahead)
+                                square_root(m, now)
+                            if m in LATE:
+                                add_root(nc.vector, m, now)
+                            else:
+                                adds.append((m, now, s))
+                    elif m not in added:
+                        raise AssertionError("logarithm before its add")
+                    elif m == last:
+                        for t in (2 * half, 2 * half + 1):
+                            logarithm(m, slice(t * M, (t + 1) * M))
+                            store(m, slice(t * M, (t + 1) * M))
+                    else:
+                        logarithm(m, halves[half])
+                        if half == 1:
+                            store(m, everything)
+                if k < TILES:
+                    sum_squares(s + AHEAD, k)
+
             spread_rows(s)
             if kind(s) == "y":
                 gram(s + 1)
             for t in range(1, TILES):
                 numerator(s, t)
             for t in range(TILES):
+                sum_squares_on_vector(s + 2, t)
                 regroup(s + 2, t)
                 if t < 2:
                     transpose(s + 2, t + 2)
@@ -453,5 +501,12 @@ def tile_hyperbolicdistancelayer_t_kernel(tc, x, y, out):
                 if s in LATE:
                     cols = slice(t * M, (t + 1) * M)
                     clip(nc.vector, s, cols)
+                if SQ_EARLY and s == last:
+                    if t == 0:
+                        new_root(s)
+                    if t > 0:
+                        square_on_vector(s, slice((t - 1) * M, t * M))
+                    if t == TILES - 1:
+                        square_on_vector(s, slice(t * M, (t + 1) * M))
                 table_slot(t)
-        assert done == len(table_work)
+        assert done == len(table_work) and not adds

@@ -28,8 +28,8 @@ COSH_MAX = (1.0 + NORM_MAX * NORM_MAX) / (1.0 - NORM_MAX * NORM_MAX)
 FLOOR = 1e-15
 ROOT_HALF = 0.5**0.5
 
-LOG_BLOCKS = (3, 4, 4, 4, 1)
-AHEAD = 5
+LOG_BLOCKS = (4, 6, 5, 1)
+AHEAD = 4
 BUD = 6
 LAG = 1
 SLOTS = 4
@@ -42,7 +42,7 @@ V_SUMS = ()
 FENCE = True
 ADDS = 2
 FIRST = 3
-CV = 0
+CV = 256
 CP = 1024
 BUD2 = 8
 KEEP = 1
@@ -53,6 +53,7 @@ SYNC_STORE = True
 GATE = True
 V_SQUARES = (17,)
 SQ_EARLY = False
+MX_AT = ((), (0, 1), (), (2, 3))
 
 
 def tile_hyperbolicdistancelayer_t_kernel(tc, x, y, out):
@@ -87,13 +88,13 @@ def tile_hyperbolicdistancelayer_t_kernel(tc, x, y, out):
 
     with (
         tc.tile_pool(name="const", bufs=1) as const,
-        tc.tile_pool(name="raw_pool", bufs=7) as raw_pool,
+        tc.tile_pool(name="raw_pool", bufs=6) as raw_pool,
         tc.tile_pool(name="grouped_pool", bufs=2) as grouped_pool,
         tc.tile_pool(name="mx_pool", bufs=2) as mx_pool,
         tc.tile_pool(name="small", bufs=8) as small,
         tc.tile_pool(name="diag_pool", bufs=2) as diag_pool,
         tc.tile_pool(name="rows_pool", bufs=2) as rows_pool,
-        tc.tile_pool(name="z_pool", bufs=11) as z_pool,
+        tc.tile_pool(name="z_pool", bufs=13) as z_pool,
         tc.tile_pool(name="root_pool", bufs=4) as root_pool,
         tc.psum_pool(name="turned_pool", bufs=2) as turned_pool,
         tc.psum_pool(name="dot_pool", bufs=4) as dot_pool,
@@ -491,10 +492,10 @@ def tile_hyperbolicdistancelayer_t_kernel(tc, x, y, out):
                 regroup(s + 2, t)
                 if t < 2:
                     transpose(s + 2, t + 2)
-                    multiply(s + 1, t)
                 else:
                     transpose(s + 3, t - 2)
-                    multiply(s + 1, t)
+                for j in MX_AT[t]:
+                    multiply(s + 1, j)
                 if t == KEEP:
                     keep_a_row(s)
                 cosh(s, t)

@@ -28,8 +28,8 @@ COSH_MAX = (1.0 + NORM_MAX * NORM_MAX) / (1.0 - NORM_MAX * NORM_MAX)
 FLOOR = 1e-15
 ROOT_HALF = 0.5**0.5
 
-LOG_BLOCKS = (4, 6, 5, 1)
-AHEAD = 4
+LOG_BLOCKS = (5, 6, 4, 1)
+AHEAD = 5
 BUD = 6
 LAG = 1
 SLOTS = 4
@@ -53,7 +53,7 @@ SYNC_STORE = True
 GATE = True
 V_SQUARES = (17,)
 SQ_EARLY = False
-MX_AT = ((), (0, 1), (), (2, 3))
+MX_AT = ((), (0, 1, 2, 3), (), ())
 
 
 def tile_hyperbolicdistancelayer_t_kernel(tc, x, y, out):
@@ -88,13 +88,13 @@ def tile_hyperbolicdistancelayer_t_kernel(tc, x, y, out):
 
     with (
         tc.tile_pool(name="const", bufs=1) as const,
-        tc.tile_pool(name="raw_pool", bufs=6) as raw_pool,
+        tc.tile_pool(name="raw_pool", bufs=7) as raw_pool,
         tc.tile_pool(name="grouped_pool", bufs=2) as grouped_pool,
         tc.tile_pool(name="mx_pool", bufs=2) as mx_pool,
         tc.tile_pool(name="small", bufs=8) as small,
         tc.tile_pool(name="diag_pool", bufs=2) as diag_pool,
         tc.tile_pool(name="rows_pool", bufs=2) as rows_pool,
-        tc.tile_pool(name="z_pool", bufs=13) as z_pool,
+        tc.tile_pool(name="z_pool", bufs=12) as z_pool,
         tc.tile_pool(name="root_pool", bufs=4) as root_pool,
         tc.psum_pool(name="turned_pool", bufs=2) as turned_pool,
         tc.psum_pool(name="dot_pool", bufs=4) as dot_pool,
@@ -110,7 +110,7 @@ def tile_hyperbolicdistancelayer_t_kernel(tc, x, y, out):
         nc.vector.memset(one[:], 1.0)
         squares = const.tile([P, 2 * D], BF16)
 
-        gram_tiles = {m: (2, 3) if m % 4 else (3,) for m in range(18) if m % 9 > 1}
+        gram_tiles = {m: (2, 3) if m % 4 or m == 16 else (3,) for m in range(18) if m % 9 > 1}
         raw = {}
         sumsq = {}
         gram_bank = {}
@@ -477,8 +477,7 @@ def tile_hyperbolicdistancelayer_t_kernel(tc, x, y, out):
                             store(m, slice(t * M, (t + 1) * M))
                     else:
                         logarithm(m, halves[half])
-                        if half == 1:
-                            store(m, everything)
+                        store(m, halves[half])
                 if k < TILES:
                     sum_squares(s + AHEAD, k)
 

import concourse.mybir as mybir
from concourse.masks import make_identity

F32 = mybir.dt.float32
BF16 = mybir.dt.bfloat16
U32 = mybir.dt.uint32
U8 = mybir.dt.uint8
FP8X4 = mybir.dt.float8_e4m3fn_x4
ALU = mybir.AluOpType
FUNC = mybir.ActivationFunctionType

B, N, M, D = 2, 4096, 512, 1024
FLOPS = 2 * B * N * M * D

P = 128
TILES = 4
ITEM_ROWS = P * TILES
GROUPS = N // ITEM_ROWS
K_PASS = 4 * P
PASSES = D // K_PASS
HALVES = 2
ROW_WORDS = D // 2
OUT_COLS = TILES * M
HALF = OUT_COLS // 2

NORM_MAX = 0.99
COSH_MAX = (1.0 + NORM_MAX * NORM_MAX) / (1.0 - NORM_MAX * NORM_MAX)
FLOOR = 1e-15
ROOT_HALF = 0.5**0.5

LOG_BLOCKS = (5, 6, 4, 1)
AHEAD = 5
BUD = 6
LAG = 1
SLOTS = 4
RG_S = ()
GP = 1024
QH = 1
LATE = (16, 17)
SPLIT = 1
V_SUMS = ()
FENCE = True
ADDS = 2
FIRST = 3
CV = 256
CP = 1024
BUD2 = 8
KEEP = 1
ADDLAG = 1
ADDS_FIRST = False
LAGGED = False
SYNC_STORE = True
GATE = True
V_SQUARES = (17,)
SQ_EARLY = False
MX_AT = ((), (0, 1, 2, 3), (), ())


def tile_hyperbolicdistancelayer_t_kernel(tc, x, y, out):
    nc = tc.nc
    STORE = nc.sync if SYNC_STORE else nc.scalar

    x_items = x.rearrange("b (g p t) k -> b g p (t k)", p=P, t=TILES)
    y_items = y.rearrange("b (t p) k -> b p t k", p=P)
    out_items = out.rearrange("b (g p t) j -> b g p (t j)", p=P, t=TILES)

    items = []
    for b in range(B):
        items.append(("y", b, 0))
        for g in range(GROUPS):
            items.append(("x", b, g))
    x_order = [m for m in range(len(items)) if items[m][0] == "x"]
    last = x_order[-1]

    table_work = []
    first = 0
    rooted = []
    for size in LOG_BLOCKS:
        block = list(range(first, first + size))
        first += size
        table_work.extend(("root", n, 0) for n in block)
        if LAGGED:
            table_work.extend(("ln", n, half) for n in rooted for half in range(2))
            rooted = block
        else:
            table_work.extend(("ln", n, half) for n in block for half in range(2))
    table_work.extend(("ln", n, half) for n in rooted for half in range(2))

    with (
        tc.tile_pool(name="const", bufs=1) as const,
        tc.tile_pool(name="raw_pool", bufs=7) as raw_pool,
        tc.tile_pool(name="grouped_pool", bufs=2) as grouped_pool,
        tc.tile_pool(name="mx_pool", bufs=2) as mx_pool,
        tc.tile_pool(name="small", bufs=8) as small,
        tc.tile_pool(name="diag_pool", bufs=2) as diag_pool,
        tc.tile_pool(name="rows_pool", bufs=2) as rows_pool,
        tc.tile_pool(name="z_pool", bufs=12) as z_pool,
        tc.tile_pool(name="root_pool", bufs=4) as root_pool,
        tc.psum_pool(name="turned_pool", bufs=2) as turned_pool,
        tc.psum_pool(name="dot_pool", bufs=4) as dot_pool,
        tc.psum_pool(name="g_pool", bufs=1) as g_pool,
        tc.psum_pool(name="gram_pool", bufs=1) as gram_pool,
        tc.manual_schedule(),
    ):
        identity = const.tile([P, P], F32)
        make_identity(nc, identity[:])
        minus_one = const.tile([P, 1], F32)
        nc.vector.memset(minus_one[:], -1.0)
        one = const.tile([P, 1], F32)
        nc.vector.memset(one[:], 1.0)
        squares = const.tile([P, 2 * D], BF16)

        gram_tiles = {m: (2, 3) if m % 4 or m == 16 else (3,) for m in range(18) if m % 9 > 1}
        raw = {}
        sumsq = {}
        gram_bank = {}
        turned = {}
        grouped = {}
        codes = {}
        scales = {}
        h_of = {}
        g_of = {}
        a_row = {}
        a_bank = {}
        g_bank = {}
        dots = {}
        z_of = {}
        root = {}
        y_of = {}

        def kind(m):
            return items[m][0] if 0 <= m < len(items) else "none"

        def load(m):
            if kind(m) == "none":
                return
            what, b, g = items[m]
            rows = raw_pool.tile([P, TILES * D], BF16)
            raw[m] = rows
            sums = small.tile([P, TILES], F32)
            sumsq[m] = sums
            if m < SPLIT:
                for t in range(TILES):
                    cols = slice(t * D, (t + 1) * D)
                    source = x_items[b, g][:, cols] if what == "x" else y_items[b][:, t]
                    nc.sync.dma_start(out=rows[:, cols], in_=source)
            elif what == "x":
                nc.sync.dma_start(out=rows[:], in_=x_items[b, g])
            else:
                nc.sync.dma_start(out=rows[:].rearrange("p (t k) -> p t k", t=TILES), in_=y_items[b])

        def by_gram(m):
            return gram_tiles.get(m, ())

        def gram(m):
            if not by_gram(m):
                return
            products = gram_pool.tile([P, TILES, P], F32)
            gram_bank[m] = products
            order = "q (c t r e) -> q c t r e" if kind(m) == "y" else "q (t c r e) -> q c t r e"
            values = grouped[m][:].rearrange(order, c=PASSES, t=TILES, r=P)
            for n, t in enumerate(by_gram(m)):
                for c in range(PASSES):
                    for e in range(4):
                        block = values[:, c, t, :, e]
                        nc.tensor.matmul(
                            out=gram_bank[m][:, n, :],
                            lhsT=block,
                            rhs=block,
                            start=(c == 0 and e == 0),
                            stop=(c == PASSES - 1 and e == 3),
                        )

        def diagonal(m):
            for n, t in enumerate(by_gram(m)):
                off = diag_pool.tile([P, P], F32)
                nc.vector.scalar_tensor_tensor(
                    out=off[:],
                    in0=gram_bank[m][:, n, :],
                    scalar=0.5,
                    in1=identity[:],
                    op0=ALU.mult,
                    op1=ALU.mult,
                    accum_out=sumsq[m][:, t : t + 1],
                )

        def sum_squares(m, t):
            if kind(m) == "none" or t in by_gram(m):
                return
            cols = slice(t * D, (t + 1) * D)
            if (m, t) in V_SUMS:
                return
            nc.scalar.activation(
                out=squares[:, t % 2 * D : (t % 2 + 1) * D],
                in_=raw[m][:, cols],
                func=FUNC.Square,
                scale=ROOT_HALF,
                accum_out=sumsq[m][:, t : t + 1],
            )

        def sum_squares_on_vector(m, t):
            if (m, t) not in V_SUMS:
                return
            cols = slice(t * D, (t + 1) * D)
            off = diag_pool.tile([P, D], BF16, tag="v_squares")
            nc.vector.scalar_tensor_tensor(
                out=off[:],
                in0=raw[m][:, cols],
                scalar=0.5,
                in1=raw[m][:, cols],
                op0=ALU.mult,
                op1=ALU.mult,
                accum_out=sumsq[m][:, t : t + 1],
            )

        def transpose(m, t):
            if kind(m) == "none":
                return
            words = raw[m][:].bitcast(F32)
            bank = turned_pool.tile([P, PASSES, HALVES, P], F32)
            turned[m, t] = bank
            for c in range(PASSES):
                for u in range(HALVES):
                    first = t * ROW_WORDS + (c * HALVES + u) * P
                    nc.tensor.transpose(bank[:, c, u, :], words[:, first : first + P], identity[:])

        def regroup(m, t):
            if kind(m) == "none":
                return
            if t == 0:
                values = grouped_pool.tile([P, TILES * D], BF16, align_bytes=64)
                grouped[m] = values
            order = "q (t c r u) -> q t c r u" if kind(m) == "x" else "q (c t r u) -> q t c r u"
            places = grouped[m][:].bitcast(F32).rearrange(order, t=TILES, c=PASSES, r=P, u=HALVES)
            copy = nc.scalar.copy if (m, t) in RG_S else nc.vector.tensor_copy
            copy(out=places[:, t], in_=turned[m, t][:].rearrange("q c u r -> q c r u"))

        def quantise(m, half):
            if kind(m) == "none":
                return
            tag = kind(m)
            if half == 0:
                packed = mx_pool.tile([P, TILES * D // 4], U32, align_bytes=64, tag=tag + "_codes")
                plane = mx_pool.tile([P, TILES * D // 4], U8, align_bytes=64, tag=tag + "_scales")
                codes[m] = packed
                scales[m] = plane
            if QH == 1 and half == 1:
                return
            w = TILES * D // QH
            cols = slice(half * w // 4, (half + 1) * w // 4)
            nc.vector.quantize_mx(
                out=codes[m][:, cols].bitcast(FP8X4),
                scales=scales[m][:, cols],
                in_=grouped[m][:, half * w : (half + 1) * w],
            )

        def factors(m, stage):
            if kind(m) == "none":
                return
            if stage == 0:
                h = small.tile([P, TILES], F32)
                h_of[m] = h
                nc.vector.tensor_scalar(
                    out=h[:], in0=sumsq[m][:], scalar1=0.5, scalar2=-FLOOR, op0=ALU.subtract, op1=ALU.min
                )
            elif stage == 2:
                g = small.tile([P, TILES], F32, tag=kind(m) + "_g")
                g_of[m] = g
                nc.vector.reciprocal(out=g[:], in_=h_of[m][:])

        def spread(bank, column):
            for t in range(TILES):
                nc.tensor.transpose(
                    bank[:, t * P : (t + 1) * P],
                    column[:, t : t + 1].to_broadcast([P, P]),
                    identity[:],
                )
            return bank

        def spread_rows(m):
            if kind(m) != "y":
                return
            acc = dot_pool.tile([P, M], F32)
            a_bank[m] = spread(acc[:], sumsq[m])
            g_row = g_pool.tile([P, M], F32)
            g_bank[m] = spread(g_row[:], g_of[m])

        def keep_a_row(m):
            if kind(m) != "y":
                return
            row = rows_pool.tile([P, M], F32)
            a_row[m] = row
            nc.vector.tensor_copy(out=row[:], in_=a_bank[m])
            y_of[items[m][1]] = m

        def multiply(m, t):
            if kind(m) != "x":
                return
            ym = codes_of_y[items[m][1]]
            acc = dot_pool.tile([P, M], F32)
            dots[m, t] = acc
            for c in range(PASSES):
                x_cols = slice((t * PASSES + c) * P, (t * PASSES + c + 1) * P)
                y_cols = slice(c * M, (c + 1) * M)
                nc.tensor.matmul_mx(
                    out=acc[:],
                    lhsT=codes[m][:, x_cols].bitcast(FP8X4),
                    lhsT_scale=scales[m][:, x_cols],
                    rhs=codes[ym][:, y_cols].bitcast(FP8X4),
                    rhs_scale=scales[ym][:, y_cols],
                    start=(c == 0),
                    stop=(c == PASSES - 1),
                )

        codes_of_y = {items[m][1]: m for m in range(len(items)) if items[m][0] == "y"}

        def numerator(m, t):
            if kind(m) != "x":
                return
            ym = y_of[items[m][1]]
            if t == 0:
                z = z_pool.tile([P, OUT_COLS], F32)
                z_of[m] = z
            nc.vector.scalar_tensor_tensor(
                out=z_of[m][:, t * M : (t + 1) * M],
                in0=a_row[ym][:],
                scalar=sumsq[m][:, t : t + 1],
                in1=dots[m, t][:],
                op0=ALU.add,
                op1=ALU.subtract,
            )

        def cosh(m, t):
            if kind(m) != "x":
                return
            ym = y_of[items[m][1]]
            cols = slice(t * M, (t + 1) * M)
            nc.vector.scalar_tensor_tensor(
                out=z_of[m][:, cols],
                in0=z_of[m][:, cols],
                scalar=g_of[m][:, t : t + 1],
                in1=g_bank[ym],
                op0=ALU.mult,
                op1=ALU.mult,
            )

        def clip(engine, m, cols):
            engine.tensor_scalar(
                out=z_of[m][:, cols],
                in0=z_of[m][:, cols],
                scalar1=COSH_MAX - 1.0,
                scalar2=0.0,
                op0=ALU.min,
                op1=ALU.max,
            )

        def new_root(m):
            r = root_pool.tile([P, OUT_COLS], F32)
            root[m] = r

        def square(m, cols):
            nc.scalar.activation(out=root[m][:, cols], in_=z_of[m][:, cols], func=FUNC.Square, bias=one[:, 0:1])

        def square_on_vector(m, cols):
            nc.vector.scalar_tensor_tensor(
                out=root[m][:, cols],
                in0=z_of[m][:, cols],
                scalar=2.0,
                in1=z_of[m][:, cols],
                op0=ALU.add,
                op1=ALU.mult,
            )

        def square_root(m, cols):
            nc.scalar.activation(
                out=root[m][:, cols], in_=root[m][:, cols], func=FUNC.Sqrt, bias=minus_one[:, 0:1]
            )

        def add_root(engine, m, cols):
            engine.tensor_tensor(
                out=z_of[m][:, cols], in0=z_of[m][:, cols], in1=root[m][:, cols], op=ALU.add
            )

        def logarithm(m, cols):
            nc.scalar.activation(out=z_of[m][:, cols], in_=z_of[m][:, cols], func=FUNC.Ln, bias=one[:, 0:1])

        def store(m, cols):
            STORE.dma_start(out=out_items[items[m][1], items[m][2]][:, cols], in_=z_of[m][:, cols])

        halves = [slice(0, HALF), slice(HALF, OUT_COLS)]
        everything = slice(0, OUT_COLS)

        def pieces(cols):
            return [slice(a, a + GP) for a in range(cols.start, cols.stop, GP)]

        done = 0
        added = set(LATE)
        adds = []
        for s in range(-2 - AHEAD, len(items) + 6):
            load(s + AHEAD + 2)
            diagonal(s)
            if kind(s) != "y":
                gram(s + 1)
            numerator(s, 0)
            factors(s, 0)
            quantise(s + 1, 0)
            quantise(s + 1, 1)
            factors(s, 2)
            if CV and kind(s - 1) == "x" and s - 1 not in LATE:
                clip(nc.vector, s - 1, slice(OUT_COLS - CV, OUT_COLS))
            if kind(s) != "none" and FENCE:
                seen = small.tile([P, TILES], F32)
                nc.gpsimd.tensor_copy(out=seen[:], in_=g_of[s][:])
            if not ADDS_FIRST:
                if kind(s - 1) == "x" and s - 1 not in LATE:
                    for a in range(0, OUT_COLS - CV, CP):
                        clip(nc.gpsimd, s - 1, slice(a, min(a + CP, OUT_COLS - CV)))
            fresh = set()
            quota = ADDS if s < last else 100
            while adds and quota > 0 and adds[0][2] <= s - ADDLAG:
                m, part, when = adds.pop(0)
                for cols in pieces(part):
                    add_root(nc.gpsimd, m, cols)
                if part == halves[1]:
                    added.add(m)
                    fresh.add(m)
                quota -= 1
            if ADDS_FIRST:
                if kind(s - 1) == "x" and s - 1 not in LATE:
                    for a in range(0, OUT_COLS - CV, CP):
                        clip(nc.gpsimd, s - 1, slice(a, min(a + CP, OUT_COLS - CV)))
            ready = sum(1 for m in x_order if m <= s - LAG or m == last and s >= last)
            share = BUD if kind(s + AHEAD) != "none" else BUD2 if s < last else 1000
            slots = [[] for k in range(SLOTS)]
            spent = 0
            while spent < share and done < len(table_work) and table_work[done][1] < ready and (s > last or table_work[done][1] < len(x_order) - 1):
                what, n, half = table_work[done]
                if what == "ln" and GATE and x_order[n] not in added:
                    break
                slot = min(spent * SLOTS // share, SLOTS - 1)
                if what == "root" and x_order[n] == s - 1 and s <= last or what == "ln" and x_order[n] in fresh:
                    slot = max(slot, FIRST)
                slot = max([slot] + [k for k in range(SLOTS) if slots[k]])
                slots[slot].append((what, x_order[n], half))
                done += 1
                spent += 4 if what == "root" else 1

            def table_slot(k):
                for what, m, half in slots[k]:
                    if what == "root":
                        if not (SQ_EARLY and m == last):
                            new_root(m)
                        quarters = [slice(t * M, (t + 1) * M) for t in range(TILES)]
                        parts = quarters if m == last else halves
                        if m in V_SQUARES:
                            if not (SQ_EARLY and m == last):
                                for now in parts:
                                    square_on_vector(m, now)
                        else:
                            square(m, parts[0])
                        for now, ahead in zip(parts, parts[1:] + parts[:1]):
                            if m in V_SQUARES:
                                nc.scalar.activation(out=root[m][:, now], in_=root[m][:, now], func=FUNC.Sqrt)
                            else:
                                if ahead != parts[0]:
                                    square(m, ahead)
                                square_root(m, now)
                            if m in LATE:
                                add_root(nc.vector, m, now)
                            else:
                                adds.append((m, now, s))
                    elif m not in added:
                        raise AssertionError("logarithm before its add")
                    elif m == last:
                        for t in (2 * half, 2 * half + 1):
                            logarithm(m, slice(t * M, (t + 1) * M))
                            store(m, slice(t * M, (t + 1) * M))
                    else:
                        logarithm(m, halves[half])
                        store(m, halves[half])
                if k < TILES:
                    sum_squares(s + AHEAD, k)

            spread_rows(s)
            if kind(s) == "y":
                gram(s + 1)
            for t in range(1, TILES):
                numerator(s, t)
            for t in range(TILES):
                sum_squares_on_vector(s + 2, t)
                regroup(s + 2, t)
                if t < 2:
                    transpose(s + 2, t + 2)
                else:
                    transpose(s + 3, t - 2)
                for j in MX_AT[t]:
                    multiply(s + 1, j)
                if t == KEEP:
                    keep_a_row(s)
                cosh(s, t)
                if s in LATE:
                    cols = slice(t * M, (t + 1) * M)
                    clip(nc.vector, s, cols)
                if SQ_EARLY and s == last:
                    if t == 0:
                        new_root(s)
                    if t > 0:
                        square_on_vector(s, slice((t - 1) * M, t * M))
                    if t == TILES - 1:
                        square_on_vector(s, slice(t * M, (t + 1) * M))
                table_slot(t)
        assert done == len(table_work) and not adds
